import numpy as np
import ml_dtypes


def mxq(x, axis, fmt="e4m3"):
    dtype, down = {"e4m3": (ml_dtypes.float8_e4m3fn, 7), "e5m2": (ml_dtypes.float8_e5m2, 14)}[fmt]
    v = np.moveaxis(np.asarray(x, np.float32).astype(ml_dtypes.bfloat16).astype(np.float64), axis, -1)
    blocks = v.reshape(v.shape[:-1] + (-1, 32))
    amax = np.abs(blocks).max(-1, keepdims=True)
    byte = np.maximum(np.where(amax > 0, np.frexp(amax)[1] - 1 + 127, 0) - down, 1)
    scale = np.exp2(byte - 127.0)
    codes = (blocks / scale).astype(np.float32).astype(dtype).astype(np.float64)
    return np.moveaxis((codes * scale).reshape(v.shape), -1, axis)


WIDE = False


def mx_kscale(k):
    if not WIDE:
        return np.ones(k)
    levels = np.array([10, -10, 5, -5, 0])
    a = np.random.permutation(np.resize(levels, k // 512 * 4)).reshape(k // 512, 4)
    idx = np.arange(k)
    return np.exp2(a[idx // 512, idx % 128 // 32])


BF16 = ml_dtypes.bfloat16


def bf(x):
    return np.asarray(x, np.float32).astype(BF16)


def f64(x):
    return np.asarray(x).astype(np.float64)


B, S, N, D, H, F = 2, 8, 64, 512, 8, 2048
EPS = 1e-5


def layer_norm(v, g, b):
    mu = v.mean(-1, keepdims=True)
    d = v - mu
    var = (d * d).mean(-1, keepdims=True)
    return d / np.sqrt(var + EPS) * g + b


def setup_inputs():
    s = mx_kscale(D)
    return {
        "sctx": bf(np.random.standard_normal((B, S, N, D)) * 0.3 * s),
        "x_ln1": bf(np.random.standard_normal((B, S, N, D))),
        "out_proj_w": bf(np.random.standard_normal((D, D)) * 1.8 / np.sqrt(D) / s[None, :]),
        "out_proj_b": bf(0.1 * np.random.standard_normal(D)),
        "lnsp_g": bf(1.0 + 0.1 * np.random.standard_normal(D)),
        "lnsp_b": bf(0.1 * np.random.standard_normal(D)),
        "ln2_g": bf(1.0 + 0.1 * np.random.standard_normal(D)),
        "ln2_b": bf(0.1 * np.random.standard_normal(D)),
        "fc1_w": bf(np.random.standard_normal((F, D)) / np.sqrt(D)),
        "fc1_b": bf(0.1 * np.random.standard_normal(F)),
    }


def reference(sctx, x_ln1, out_proj_w, out_proj_b, lnsp_g, lnsp_b, ln2_g, ln2_b, fc1_w, fc1_b):
    xr = f64(x_ln1)
    sattn = (mxq(f64(sctx), 3, "e4m3") @ mxq(f64(out_proj_w), 1, "e4m3").T) + f64(out_proj_b)
    spatial_out = layer_norm(xr + sattn, f64(lnsp_g), f64(lnsp_b))
    x2 = layer_norm(xr + spatial_out, f64(ln2_g), f64(ln2_b))
    h = np.maximum((mxq(x2, 3, "e4m3") @ mxq(f64(fc1_w), 1, "e4m3").T) + f64(fc1_b), 0.0)
    return x2, h

@@ -1,0 +1,271 @@
+from contextlib import ExitStack
+
+import concourse.mybir as mybir
+from concourse.masks import make_identity
+
+F32 = mybir.dt.float32
+BF16 = mybir.dt.bfloat16
+U32 = mybir.dt.uint32
+U8 = mybir.dt.uint8
+FP8X4 = mybir.dt.float8_e4m3fn_x4
+ADD = mybir.AluOpType.add
+MULT = mybir.AluOpType.mult
+ACT = mybir.ActivationFunctionType
+
+P = 128
+D = 512
+F = 2048
+TOKENS = 1024
+EPS = 1e-5
+TILES = TOKENS // P
+PAIRS = TILES // 2
+BANK = 512
+F_BANKS = F // BANK
+
+FLOPS = 2 * TOKENS * D * (D + F)
+
+B_OUT, G_SP, B_SP, G_2, B_2 = 0, 1, 2, 3, 4
+
+
+def tile_mlcablock_pb_kernel(
+    tc, sctx, x_ln1, out_proj_w, out_proj_b, lnsp_g, lnsp_b, ln2_g, ln2_b, fc1_w, fc1_b, out_0, out_1
+):
+    nc = tc.nc
+
+    sctx_v = sctx.flatten_outer_dims().rearrange("(p t) d -> p t d", t=TILES)
+    x_v = x_ln1.flatten_outer_dims().rearrange("(p t) d -> p t d", t=TILES)
+    x2_v = out_0.flatten_outer_dims().rearrange("(p t) d -> p t d", t=TILES)
+    h_v = out_1.flatten_outer_dims().rearrange("(p t) f -> p t f", t=TILES)
+    wo_v = out_proj_w.rearrange("(r p) k -> p r k", p=P)
+    w1_v = fc1_w.rearrange("(r p) k -> p r k", p=P)
+
+    with ExitStack() as ctx:
+        keep = ctx.enter_context(tc.tile_pool(name="keep", bufs=1))
+        work = ctx.enter_context(tc.tile_pool(name="work", bufs=2))
+        stat = ctx.enter_context(tc.tile_pool(name="stat", bufs=2))
+        junk = ctx.enter_context(tc.tile_pool(name="junk", bufs=4))
+        hout = ctx.enter_context(tc.tile_pool(name="hout", bufs=4))
+        turn_ps = ctx.enter_context(tc.psum_pool(name="turn_ps", bufs=2))
+        a_ps = ctx.enter_context(tc.psum_pool(name="a_ps", bufs=2))
+        acc_ps = ctx.enter_context(tc.psum_pool(name="acc_ps", bufs=4))
+
+        ln_rows = keep.tile([P, D], BF16)
+        nc.vector.memset(ln_rows[:], 0.0)
+        eps = keep.tile([P, 1], F32)
+        nc.vector.memset(eps[:], EPS)
+        warm = keep.tile([P, 1], F32)
+        nc.scalar.activation(out=warm[:], in_=eps[:], func=ACT.Sqrt)
+        ident = keep.tile([P, P], F32)
+        make_identity(nc, ident[:])
+        ident_bf = keep.tile([P, P], BF16)
+        make_identity(nc, ident_bf[:])
+
+        wo_sb = keep.tile([P, D // P, D], BF16)
+        sctx_sb = keep.tile([P, TILES, D], BF16)
+        x_sb = keep.tile([P, TILES, D], BF16)
+        w1_sb = keep.tile([P, F // P, D], BF16)
+        nc.sync.dma_start(out=sctx_sb[:, 0:2, :], in_=sctx_v[:, 0:2, :])
+        nc.sync.dma_start(out=wo_sb[:], in_=wo_v)
+        for n, vec in enumerate((out_proj_b, lnsp_g, lnsp_b, ln2_g, ln2_b)):
+            nc.sync.dma_start(out=ln_rows[n : n + 1, :], in_=vec.rearrange("(o d) -> o d", o=1))
+        nc.sync.dma_start(out=x_sb[:, 0:2, :], in_=x_v[:, 0:2, :])
+        for q in range(F_BANKS):
+            nc.sync.dma_start(out=w1_sb[:, 4 * q : 4 * q + 4, :], in_=w1_v[:, 4 * q : 4 * q + 4, :])
+        nc.sync.dma_start(out=sctx_sb[:, 2:TILES, :], in_=sctx_v[:, 2:TILES, :])
+        nc.sync.dma_start(out=x_sb[:, 2:TILES, :], in_=x_v[:, 2:TILES, :])
+        fc1b_bc = keep.tile([P, F], BF16)
+        nc.sync.dma_start(out=fc1b_bc[:], in_=fc1_b.partition_broadcast(P))
+
+        ln_bc = keep.tile([P, 5, D], F32)
+        xb_out = keep.tile([P, TILES, D], F32)
+        xb_sp = keep.tile([P, TILES, D], F32)
+        wo_grouped = keep.tile([P, D * 4], BF16, align_bytes=64)
+        wo_codes = keep.tile([P, D], U32, align_bytes=64)
+        wo_scales = keep.tile([P, D], U8, align_bytes=64)
+        sctx_grouped = keep.tile([P, TOKENS * 4], BF16, align_bytes=64)
+        sctx_codes = keep.tile([P, TOKENS], U32, align_bytes=64)
+        sctx_scales = keep.tile([P, TOKENS], U8, align_bytes=64)
+        w1_grouped = keep.tile([P, F * 4], BF16, align_bytes=64)
+        w1_codes = keep.tile([P, F], U32, align_bytes=64)
+        w1_scales = keep.tile([P, F], U8, align_bytes=64)
+
+        def broadcast_row(n):
+            spread = acc_ps.tile([P, BANK], F32, tag="acc")
+            nc.tensor.matmul(
+                out=spread[:], lhsT=ident_bf[:, n : n + 1].to_broadcast([P, P]), rhs=ln_rows[:], start=True, stop=True
+            )
+            nc.scalar.copy(out=ln_bc[:, n, :], in_=spread[:])
+
+        def turn_two_row_tiles(rows_sb, r0, grouped):
+            turned = turn_ps.tile([P, 2, 2, P], F32, tag="turned")
+            for r in range(2):
+                words = rows_sb[:, r0 + r, :].bitcast(F32)
+                for u in range(2):
+                    nc.tensor.transpose(turned[:, r, u, :], words[:, u * P : (u + 1) * P], ident[:])
+            nc.scalar.copy(
+                out=grouped[:, r0 * P * 4 : (r0 + 2) * P * 4].bitcast(F32).rearrange("p (r c u) -> p r c u", r=2, u=2),
+                in_=turned[:].rearrange("p r u c -> p r c u"),
+            )
+
+        def quantise(grouped, codes, scales, first, count):
+            nc.vector.quantize_mx(
+                out=codes[:, first : first + count].bitcast(FP8X4),
+                scales=scales[:, first : first + count],
+                in_=grouped[:, 4 * first : 4 * (first + count)],
+            )
+
+        def prepare_sctx_pair(j):
+            turn_two_row_tiles(sctx_sb, 2 * j, sctx_grouped)
+            quantise(sctx_grouped, sctx_codes, sctx_scales, 2 * j * P, 2 * P)
+
+        def prepare_fc1_bank(c):
+            turn_two_row_tiles(w1_sb, 4 * c, w1_grouped)
+            turn_two_row_tiles(w1_sb, 4 * c + 2, w1_grouped)
+            quantise(w1_grouped, w1_codes, w1_scales, c * BANK, BANK)
+
+        def add_bias_to_residual(i):
+            nc.gpsimd.tensor_tensor(out=xb_out[:, i, :], in0=x_sb[:, i, :], in1=ln_bc[:, B_OUT, :], op=ADD)
+            nc.gpsimd.tensor_tensor(out=xb_sp[:, i, :], in0=x_sb[:, i, :], in1=ln_bc[:, B_SP, :], op=ADD)
+
+        prepare_sctx_pair(0)
+        broadcast_row(B_OUT)
+        turn_two_row_tiles(wo_sb, 0, wo_grouped)
+        turn_two_row_tiles(wo_sb, 2, wo_grouped)
+        quantise(wo_grouped, wo_codes, wo_scales, 0, D)
+        broadcast_row(G_SP)
+        broadcast_row(B_SP)
+        for i in range(TILES):
+            add_bias_to_residual(i)
+
+        def centre(v, total, gain):
+            neg_mean = stat.tile([P, 2], F32, tag="neg_mean")
+            nc.vector.tensor_scalar(out=neg_mean[:], in0=total[:], scalar1=-1.0 / D, scalar2=None, op0=MULT)
+            sum_sq = stat.tile([P, 2], F32, tag="sum_sq")
+            w = work.tile([P, 2, D], F32, tag="w")
+            for k in range(2):
+                squares = junk.tile([P, D], BF16, tag="squares")
+                nc.scalar.activation(
+                    out=squares[:], in_=v[:, k, :], func=ACT.Square, bias=neg_mean[:, k : k + 1], scale=1.0,
+                    accum_out=sum_sq[:, k : k + 1],
+                )
+            for k in range(2):
+                nc.vector.scalar_tensor_tensor(
+                    out=w[:, k, :], in0=v[:, k, :], scalar=neg_mean[:, k : k + 1], in1=ln_bc[:, gain, :],
+                    op0=ADD, op1=MULT,
+                )
+            std = stat.tile([P, 2], F32, tag="std")
+            nc.scalar.activation(out=std[:], in_=sum_sq[:], func=ACT.Sqrt, bias=eps[:], scale=1.0 / D)
+            return w, std
+
+        state = {}
+
+        def part_a(j):
+            v1 = work.tile([P, 2, D], F32, tag="v1")
+            total1 = stat.tile([P, 2], F32, tag="total1")
+            for k in range(2):
+                i = 2 * j + k
+                a = a_ps.tile([P, D], F32, tag="a")
+                nc.tensor.matmul_mx(
+                    out=a[:],
+                    lhsT=sctx_codes[:, i * P : (i + 1) * P].bitcast(FP8X4),
+                    lhsT_scale=sctx_scales[:, i * P : (i + 1) * P],
+                    rhs=wo_codes[:].bitcast(FP8X4),
+                    rhs_scale=wo_scales[:],
+                    start=True,
+                    stop=True,
+                )
+                nc.vector.scalar_tensor_tensor(
+                    out=v1[:, k, :], in0=a[:], scalar=1.0, in1=xb_out[:, i, :], op0=MULT, op1=ADD,
+                    accum_out=total1[:, k : k + 1],
+                )
+            state["w1"], state["std1"] = centre(v1, total1, G_SP)
+
+        def part_b(j):
+            rstd1 = stat.tile([P, 2], F32, tag="rstd1")
+            nc.vector.reciprocal(out=rstd1[:], in_=state["std1"][:])
+            v2 = work.tile([P, 2, D], F32, tag="v2")
+            total2 = stat.tile([P, 2], F32, tag="total2")
+            for k in range(2):
+                nc.vector.scalar_tensor_tensor(
+                    out=v2[:, k, :], in0=state["w1"][:, k, :], scalar=rstd1[:, k : k + 1], in1=xb_sp[:, 2 * j + k, :],
+                    op0=MULT, op1=ADD, accum_out=total2[:, k : k + 1],
+                )
+            state["w2"], state["std2"] = centre(v2, total2, G_2)
+
+        def part_c(j):
+            rstd2 = stat.tile([P, 2], F32, tag="rstd2")
+            nc.vector.reciprocal(out=rstd2[:], in_=state["std2"][:])
+            x2 = work.tile([P, 2, D], F32, tag="x2")
+            x2_grouped = work.tile([P, 2, P, 4], BF16, tag="x2_grouped", align_bytes=64)
+            for k in range(2):
+                nc.vector.scalar_tensor_tensor(
+                    out=x2[:, k, :], in0=state["w2"][:, k, :], scalar=rstd2[:, k : k + 1], in1=ln_bc[:, B_2, :],
+                    op0=MULT, op1=ADD,
+                )
+            nc.sync.dma_start(out=x2_v[:, 2 * j : 2 * j + 2, :], in_=x2[:])
+            for k in range(2):
+                columns = x2[:, k, :].rearrange("p (u c e) -> p u e c", u=2, e=2)
+                turned = turn_ps.tile([P, 4, P], F32, tag="turned")
+                for u in range(2):
+                    for e in range(2):
+                        nc.tensor.transpose(turned[:, 2 * u + e, :], columns[:, u, e, :], ident[:])
+                nc.scalar.copy(out=x2_grouped[:, k, :, :], in_=turned[:].rearrange("p t c -> p c t"))
+            state["x2_grouped"] = x2_grouped
+
+        def part_d(j):
+            x2_codes = work.tile([P, 2 * P], U32, tag="x2_codes", align_bytes=64)
+            x2_scales = work.tile([P, 2 * P], U8, tag="x2_scales", align_bytes=64)
+            nc.vector.quantize_mx(
+                out=x2_codes[:].bitcast(FP8X4),
+                scales=x2_scales[:],
+                in_=state["x2_grouped"][:].rearrange("p k c t -> p (k c t)"),
+            )
+            state["x2_codes", j] = x2_codes
+            state["x2_scales", j] = x2_scales
+
+        def mlp_quarter(j, q):
+            k, half = q // 2, q % 2
+            h_sb = hout.tile([P, 2, BANK], F32, tag="h_sb")
+            for b in range(2):
+                c = 2 * half + b
+                acc = acc_ps.tile([P, BANK], F32, tag="acc")
+                nc.tensor.matmul_mx(
+                    out=acc[:],
+                    lhsT=state["x2_codes", j][:, k * P : (k + 1) * P].bitcast(FP8X4),
+                    lhsT_scale=state["x2_scales", j][:, k * P : (k + 1) * P],
+                    rhs=w1_codes[:, c * BANK : (c + 1) * BANK].bitcast(FP8X4),
+                    rhs_scale=w1_scales[:, c * BANK : (c + 1) * BANK],
+                    start=True,
+                    stop=True,
+                )
+                nc.vector.tensor_tensor(out=h_sb[:, b, :], in0=acc[:], in1=fc1b_bc[:, c * BANK : (c + 1) * BANK], op=ADD)
+            nc.scalar.activation(out=h_sb[:], in_=h_sb[:], func=ACT.Relu)
+            nc.sync.dma_start(
+                out=h_v[:, 2 * j + k, 2 * half * BANK : 2 * (half + 1) * BANK],
+                in_=h_sb[:].rearrange("p b n -> p (b n)"),
+            )
+
+        def filler(j, q):
+            if j == 0:
+                prepare_fc1_bank(q)
+                if q > 0:
+                    prepare_sctx_pair(q)
+            else:
+                mlp_quarter(j - 1, q)
+
+        for j in range(PAIRS + 1):
+            if j < PAIRS:
+                part_a(j)
+            if j == 0:
+                broadcast_row(G_2)
+                broadcast_row(B_2)
+            filler(j, 0)
+            if j < PAIRS:
+                part_b(j)
+            filler(j, 1)
+            if j < PAIRS:
+                part_c(j)
+            filler(j, 2)
+            filler(j, 3)
+            if j < PAIRS:
+                part_d(j)

@@ -18,9 +18,12 @@ F = 2048
 TOKENS = 1024
 EPS = 1e-5
 TILES = TOKENS // P
-PAIRS = TILES // 2
+HALF = TILES // 2
 BANK = 512
 F_BANKS = F // BANK
+H_BANKS = TILES * F_BANKS
+AHEAD = 3
+H_BUFS = 10
 
 FLOPS = 2 * TOKENS * D * (D + F)
 
@@ -37,235 +40,295 @@ def tile_mlcablock_pb_kernel(
     x2_v = out_0.flatten_outer_dims().rearrange("(p t) d -> p t d", t=TILES)
     h_v = out_1.flatten_outer_dims().rearrange("(p t) f -> p t f", t=TILES)
     wo_v = out_proj_w.rearrange("(r p) k -> p r k", p=P)
-    w1_v = fc1_w.rearrange("(r p) k -> p r k", p=P)
+    fc1_v = fc1_w.rearrange("(r p) k -> p r k", p=P)
 
     with ExitStack() as ctx:
+        ctx.enter_context(tc.manual_schedule())
         keep = ctx.enter_context(tc.tile_pool(name="keep", bufs=1))
-        work = ctx.enter_context(tc.tile_pool(name="work", bufs=2))
-        stat = ctx.enter_context(tc.tile_pool(name="stat", bufs=2))
-        junk = ctx.enter_context(tc.tile_pool(name="junk", bufs=4))
-        hout = ctx.enter_context(tc.tile_pool(name="hout", bufs=4))
-        turn_ps = ctx.enter_context(tc.psum_pool(name="turn_ps", bufs=2))
-        a_ps = ctx.enter_context(tc.psum_pool(name="a_ps", bufs=2))
-        acc_ps = ctx.enter_context(tc.psum_pool(name="acc_ps", bufs=4))
-
-        ln_rows = keep.tile([P, D], BF16)
-        nc.vector.memset(ln_rows[:], 0.0)
-        eps = keep.tile([P, 1], F32)
-        nc.vector.memset(eps[:], EPS)
-        warm = keep.tile([P, 1], F32)
-        nc.scalar.activation(out=warm[:], in_=eps[:], func=ACT.Sqrt)
-        ident = keep.tile([P, P], F32)
-        make_identity(nc, ident[:])
-        ident_bf = keep.tile([P, P], BF16)
-        make_identity(nc, ident_bf[:])
-
-        wo_sb = keep.tile([P, D // P, D], BF16)
-        sctx_sb = keep.tile([P, TILES, D], BF16)
-        x_sb = keep.tile([P, TILES, D], BF16)
-        w1_sb = keep.tile([P, F // P, D], BF16)
-        nc.sync.dma_start(out=sctx_sb[:, 0:2, :], in_=sctx_v[:, 0:2, :])
-        nc.sync.dma_start(out=wo_sb[:], in_=wo_v)
-        for n, vec in enumerate((out_proj_b, lnsp_g, lnsp_b, ln2_g, ln2_b)):
-            nc.sync.dma_start(out=ln_rows[n : n + 1, :], in_=vec.rearrange("(o d) -> o d", o=1))
-        nc.sync.dma_start(out=x_sb[:, 0:2, :], in_=x_v[:, 0:2, :])
-        for q in range(F_BANKS):
-            nc.sync.dma_start(out=w1_sb[:, 4 * q : 4 * q + 4, :], in_=w1_v[:, 4 * q : 4 * q + 4, :])
-        nc.sync.dma_start(out=sctx_sb[:, 2:TILES, :], in_=sctx_v[:, 2:TILES, :])
-        nc.sync.dma_start(out=x_sb[:, 2:TILES, :], in_=x_v[:, 2:TILES, :])
+        psum = ctx.enter_context(tc.psum_pool(name="psum", bufs=8))
+        fc1_codes = keep.tile([P, F], U32, align_bytes=64)
+        fc1_scales = keep.tile([P, F], U8, align_bytes=64)
         fc1b_bc = keep.tile([P, F], BF16)
-        nc.sync.dma_start(out=fc1b_bc[:], in_=fc1_b.partition_broadcast(P))
+        live = {}
+        for half in range(2):
+            live["x2_codes", half] = keep.tile([P, HALF * P], U32, name="x2_codes_%d" % half, align_bytes=64)
+            live["x2_scales", half] = keep.tile([P, HALF * P], U8, name="x2_scales_%d" % half, align_bytes=64)
 
-        ln_bc = keep.tile([P, 5, D], F32)
-        xb_out = keep.tile([P, TILES, D], F32)
-        xb_sp = keep.tile([P, TILES, D], F32)
-        wo_grouped = keep.tile([P, D * 4], BF16, align_bytes=64)
-        wo_codes = keep.tile([P, D], U32, align_bytes=64)
-        wo_scales = keep.tile([P, D], U8, align_bytes=64)
-        sctx_grouped = keep.tile([P, TOKENS * 4], BF16, align_bytes=64)
-        sctx_codes = keep.tile([P, TOKENS], U32, align_bytes=64)
-        sctx_scales = keep.tile([P, TOKENS], U8, align_bytes=64)
-        w1_grouped = keep.tile([P, F * 4], BF16, align_bytes=64)
-        w1_codes = keep.tile([P, F], U32, align_bytes=64)
-        w1_scales = keep.tile([P, F], U8, align_bytes=64)
+        with ExitStack() as early:
+            prep = early.enter_context(tc.tile_pool(name="prep", bufs=1))
+            work = early.enter_context(tc.tile_pool(name="work", bufs=1))
+            turn = early.enter_context(tc.tile_pool(name="turn", bufs=2))
+            stat = early.enter_context(tc.tile_pool(name="stat", bufs=2))
+            junk = early.enter_context(tc.tile_pool(name="junk", bufs=4))
 
-        def broadcast_row(n):
-            spread = acc_ps.tile([P, BANK], F32, tag="acc")
-            nc.tensor.matmul(
-                out=spread[:], lhsT=ident_bf[:, n : n + 1].to_broadcast([P, P]), rhs=ln_rows[:], start=True, stop=True
-            )
-            nc.scalar.copy(out=ln_bc[:, n, :], in_=spread[:])
+            ln_rows = prep.tile([P, D], BF16)
+            nc.vector.memset(ln_rows[:], 0.0)
+            eps = prep.tile([P, 1], F32)
+            nc.vector.memset(eps[:], EPS)
+            warm = prep.tile([P, 1], F32)
+            nc.scalar.activation(out=warm[:], in_=eps[:], func=ACT.Sqrt)
+            ident = prep.tile([P, P], F32)
+            make_identity(nc, ident[:])
+            ident_bf = prep.tile([P, P], BF16)
+            make_identity(nc, ident_bf[:])
 
-        def turn_two_row_tiles(rows_sb, r0, grouped):
-            turned = turn_ps.tile([P, 2, 2, P], F32, tag="turned")
-            for r in range(2):
-                words = rows_sb[:, r0 + r, :].bitcast(F32)
-                for u in range(2):
-                    nc.tensor.transpose(turned[:, r, u, :], words[:, u * P : (u + 1) * P], ident[:])
-            nc.scalar.copy(
-                out=grouped[:, r0 * P * 4 : (r0 + 2) * P * 4].bitcast(F32).rearrange("p (r c u) -> p r c u", r=2, u=2),
-                in_=turned[:].rearrange("p r u c -> p r c u"),
-            )
+            wo_sb = prep.tile([P, D // P, D], BF16)
+            sctx_sb = prep.tile([P, TILES, D], BF16)
+            x_sb = prep.tile([P, TILES, D], BF16)
+            fc1_sb = prep.tile([P, F // P, D], BF16)
+            nc.sync.dma_start(out=sctx_sb[:, 0:2, :], in_=sctx_v[:, 0:2, :])
+            nc.sync.dma_start(out=wo_sb[:], in_=wo_v)
+            for n, vec in enumerate((out_proj_b, lnsp_g, lnsp_b, ln2_g, ln2_b)):
+                nc.sync.dma_start(out=ln_rows[n : n + 1, :], in_=vec.rearrange("(o d) -> o d", o=1))
+            nc.sync.dma_start(out=x_sb[:, 0:2, :], in_=x_v[:, 0:2, :])
+            nc.sync.dma_start(out=sctx_sb[:, 2:HALF, :], in_=sctx_v[:, 2:HALF, :])
+            nc.sync.dma_start(out=x_sb[:, 2:HALF, :], in_=x_v[:, 2:HALF, :])
+            nc.sync.dma_start(out=sctx_sb[:, HALF:TILES, :], in_=sctx_v[:, HALF:TILES, :])
+            nc.sync.dma_start(out=x_sb[:, HALF:TILES, :], in_=x_v[:, HALF:TILES, :])
+            for c in range(F_BANKS):
+                nc.sync.dma_start(out=fc1_sb[:, 4 * c : 4 * c + 4, :], in_=fc1_v[:, 4 * c : 4 * c + 4, :])
+            nc.sync.dma_start(out=fc1b_bc[:], in_=fc1_b.partition_broadcast(P))
 
-        def quantise(grouped, codes, scales, first, count):
-            nc.vector.quantize_mx(
-                out=codes[:, first : first + count].bitcast(FP8X4),
-                scales=scales[:, first : first + count],
-                in_=grouped[:, 4 * first : 4 * (first + count)],
-            )
+            ln_bc = prep.tile([P, 5, D], F32)
+            xb_out = prep.tile([P, TILES, D], F32)
+            xb_sp = prep.tile([P, TILES, D], F32)
+            wo_grouped = prep.tile([P, D * 4], BF16, align_bytes=64)
+            wo_codes = prep.tile([P, D], U32, align_bytes=64)
+            wo_scales = prep.tile([P, D], U8, align_bytes=64)
+            sctx_grouped = prep.tile([P, TOKENS * 4], BF16, align_bytes=64)
+            sctx_codes = prep.tile([P, TOKENS], U32, align_bytes=64)
+            sctx_scales = prep.tile([P, TOKENS], U8, align_bytes=64)
+            fc1_grouped = prep.tile([P, F * 4], BF16, align_bytes=64)
 
-        def prepare_sctx_pair(j):
-            turn_two_row_tiles(sctx_sb, 2 * j, sctx_grouped)
-            quantise(sctx_grouped, sctx_codes, sctx_scales, 2 * j * P, 2 * P)
+            def broadcast_row(n):
+                spread = psum.tile([P, BANK], F32, tag="bank")
+                nc.tensor.matmul(
+                    out=spread[:], lhsT=ident_bf[:, n : n + 1].to_broadcast([P, P]), rhs=ln_rows[:], start=True, stop=True
+                )
+                nc.scalar.copy(out=ln_bc[:, n, :], in_=spread[:])
 
-        def prepare_fc1_bank(c):
-            turn_two_row_tiles(w1_sb, 4 * c, w1_grouped)
-            turn_two_row_tiles(w1_sb, 4 * c + 2, w1_grouped)
-            quantise(w1_grouped, w1_codes, w1_scales, c * BANK, BANK)
+            def turn_two_row_tiles(rows_sb, r0, grouped):
+                turned = psum.tile([P, 2, 2, P], F32, tag="bank")
+                for r in range(2):
+                    words = rows_sb[:, r0 + r, :].bitcast(F32)
+                    for u in range(2):
+                        nc.tensor.transpose(turned[:, r, u, :], words[:, u * P : (u + 1) * P], ident[:])
+                nc.scalar.copy(
+                    out=grouped[:, r0 * P * 4 : (r0 + 2) * P * 4].bitcast(F32).rearrange("p (r c u) -> p r c u", r=2, u=2),
+                    in_=turned[:].rearrange("p r u c -> p r c u"),
+                )
 
-        def add_bias_to_residual(i):
-            nc.gpsimd.tensor_tensor(out=xb_out[:, i, :], in0=x_sb[:, i, :], in1=ln_bc[:, B_OUT, :], op=ADD)
-            nc.gpsimd.tensor_tensor(out=xb_sp[:, i, :], in0=x_sb[:, i, :], in1=ln_bc[:, B_SP, :], op=ADD)
+            def quantise(grouped, codes, scales, first, count):
+                nc.vector.quantize_mx(
+                    out=codes[:, first : first + count].bitcast(FP8X4),
+                    scales=scales[:, first : first + count],
+                    in_=grouped[:, 4 * first : 4 * (first + count)],
+                )
 
-        prepare_sctx_pair(0)
-        broadcast_row(B_OUT)
-        turn_two_row_tiles(wo_sb, 0, wo_grouped)
-        turn_two_row_tiles(wo_sb, 2, wo_grouped)
-        quantise(wo_grouped, wo_codes, wo_scales, 0, D)
-        broadcast_row(G_SP)
-        broadcast_row(B_SP)
-        for i in range(TILES):
-            add_bias_to_residual(i)
+            def turn_sctx_pair(j):
+                turn_two_row_tiles(sctx_sb, 2 * j, sctx_grouped)
 
-        def centre(v, total, gain):
-            neg_mean = stat.tile([P, 2], F32, tag="neg_mean")
-            nc.vector.tensor_scalar(out=neg_mean[:], in0=total[:], scalar1=-1.0 / D, scalar2=None, op0=MULT)
-            sum_sq = stat.tile([P, 2], F32, tag="sum_sq")
-            w = work.tile([P, 2, D], F32, tag="w")
-            for k in range(2):
-                squares = junk.tile([P, D], BF16, tag="squares")
+            def quantise_sctx_pair(j):
+                quantise(sctx_grouped, sctx_codes, sctx_scales, 2 * j * P, 2 * P)
+
+            def turn_fc1_half_bank(b):
+                turn_two_row_tiles(fc1_sb, 2 * b, fc1_grouped)
+
+            def quantise_fc1_bank(c):
+                quantise(fc1_grouped, fc1_codes, fc1_scales, c * BANK, BANK)
+
+            def open_norm():
+                total = stat.tile([P, HALF], F32, tag="total")
+                neg_mean = stat.tile([P, HALF], F32, tag="neg_mean")
+                sum_sq = stat.tile([P, HALF], F32, tag="sum_sq")
+                std = stat.tile([P, HALF], F32, tag="std")
+                rstd = stat.tile([P, HALF], F32, tag="rstd")
+                return {"total": total, "neg_mean": neg_mean, "sum_sq": sum_sq, "std": std, "rstd": rstd}
+
+            def pair_statistics(norm, v, m):
+                pair = slice(2 * m, 2 * m + 2)
+                nc.vector.tensor_scalar(
+                    out=norm["neg_mean"][:, pair], in0=norm["total"][:, pair], scalar1=-1.0 / D, scalar2=None, op0=MULT
+                )
+                for k in (2 * m, 2 * m + 1):
+                    squares = junk.tile([P, D], BF16, tag="squares")
+                    nc.scalar.activation(
+                        out=squares[:], in_=v[:, k, :], func=ACT.Square, bias=norm["neg_mean"][:, k : k + 1], scale=1.0,
+                        accum_out=norm["sum_sq"][:, k : k + 1],
+                    )
                 nc.scalar.activation(
-                    out=squares[:], in_=v[:, k, :], func=ACT.Square, bias=neg_mean[:, k : k + 1], scale=1.0,
-                    accum_out=sum_sq[:, k : k + 1],
+                    out=norm["std"][:, pair], in_=norm["sum_sq"][:, pair], func=ACT.Sqrt, bias=eps[:], scale=1.0 / D
                 )
-            for k in range(2):
-                nc.vector.scalar_tensor_tensor(
-                    out=w[:, k, :], in0=v[:, k, :], scalar=neg_mean[:, k : k + 1], in1=ln_bc[:, gain, :],
-                    op0=ADD, op1=MULT,
+
+            def pair_reciprocal(norm, m):
+                pair = slice(2 * m, 2 * m + 2)
+                nc.vector.reciprocal(out=norm["rstd"][:, pair], in_=norm["std"][:, pair])
+
+            def first_residual(half, norm, v1, m):
+                for k in (2 * m, 2 * m + 1):
+                    i = HALF * half + k
+                    a = psum.tile([P, D], F32, tag="bank")
+                    nc.tensor.matmul_mx(
+                        out=a[:],
+                        lhsT=sctx_codes[:, i * P : (i + 1) * P].bitcast(FP8X4),
+                        lhsT_scale=sctx_scales[:, i * P : (i + 1) * P],
+                        rhs=wo_codes[:].bitcast(FP8X4),
+                        rhs_scale=wo_scales[:],
+                        start=True,
+                        stop=True,
+                    )
+                    nc.vector.scalar_tensor_tensor(
+                        out=v1[:, k, :], in0=a[:], scalar=1.0, in1=xb_out[:, i, :], op0=MULT, op1=ADD,
+                        accum_out=norm["total"][:, k : k + 1],
+                    )
+                pair_statistics(norm, v1, m)
+
+            def centre_and_gain(norm, v, gain, w):
+                for k in range(HALF):
+                    nc.vector.scalar_tensor_tensor(
+                        out=w[:, k, :], in0=v[:, k, :], scalar=norm["neg_mean"][:, k : k + 1], in1=ln_bc[:, gain, :],
+                        op0=ADD, op1=MULT,
+                    )
+
+            def second_residual(half, norm1, w1, norm2, v2, m):
+                pair_reciprocal(norm1, m)
+                for k in (2 * m, 2 * m + 1):
+                    nc.vector.scalar_tensor_tensor(
+                        out=v2[:, k, :], in0=w1[:, k, :], scalar=norm1["rstd"][:, k : k + 1],
+                        in1=xb_sp[:, HALF * half + k, :], op0=MULT, op1=ADD, accum_out=norm2["total"][:, k : k + 1],
+                    )
+                pair_statistics(norm2, v2, m)
+
+            def finish_x2(half, norm2, w2, x2, x2_grouped, m):
+                pair_reciprocal(norm2, m)
+                for k in (2 * m, 2 * m + 1):
+                    nc.vector.scalar_tensor_tensor(
+                        out=x2[:, k, :], in0=w2[:, k, :], scalar=norm2["rstd"][:, k : k + 1], in1=ln_bc[:, B_2, :],
+                        op0=MULT, op1=ADD,
+                    )
+                first = HALF * half + 2 * m
+                nc.sync.dma_start(out=x2_v[:, first : first + 2, :], in_=x2[:, 2 * m : 2 * m + 2, :])
+                for k in (2 * m, 2 * m + 1):
+                    columns = x2[:, k, :].rearrange("p (u c e) -> p u e c", u=2, e=2)
+                    turned = psum.tile([P, 4, P], F32, tag="bank")
+                    for u in range(2):
+                        for e in range(2):
+                            nc.tensor.transpose(turned[:, 2 * u + e, :], columns[:, u, e, :], ident[:])
+                    nc.scalar.copy(out=x2_grouped[:, k, :, :], in_=turned[:].rearrange("p t c -> p c t"))
+
+            def layer_norms(half, scalar_spare_1, scalar_spare_2):
+                norm1 = open_norm()
+                norm2 = open_norm()
+                v1 = work.tile([P, HALF, D], F32, tag="v1")
+                w1 = work.tile([P, HALF, D], F32, tag="w")
+                v2 = work.tile([P, HALF, D], F32, tag="v2")
+                x2 = turn.tile([P, HALF, D], F32, tag="x2")
+                x2_grouped = turn.tile([P, HALF, P, 4], BF16, tag="x2_grouped", align_bytes=64)
+                first_residual(half, norm1, v1, 0)
+                first_residual(half, norm1, v1, 1)
+                centre_and_gain(norm1, v1, G_SP, w1)
+                scalar_spare_1()
+                second_residual(half, norm1, w1, norm2, v2, 0)
+                second_residual(half, norm1, w1, norm2, v2, 1)
+                w2 = work.tile([P, HALF, D], F32, tag="w")
+                centre_and_gain(norm2, v2, G_2, w2)
+                scalar_spare_2()
+                finish_x2(half, norm2, w2, x2, x2_grouped, 0)
+                finish_x2(half, norm2, w2, x2, x2_grouped, 1)
+                return x2_grouped
+
+            def quantise_x2(half, x2_grouped):
+                nc.vector.quantize_mx(
+                    out=live["x2_codes", half][:].bitcast(FP8X4),
+                    scales=live["x2_scales", half][:],
+                    in_=x2_grouped[:].rearrange("p k c t -> p (k c t)"),
                 )
-            std = stat.tile([P, 2], F32, tag="std")
-            nc.scalar.activation(out=std[:], in_=sum_sq[:], func=ACT.Sqrt, bias=eps[:], scale=1.0 / D)
-            return w, std
 
-        state = {}
-
-        def part_a(j):
-            v1 = work.tile([P, 2, D], F32, tag="v1")
-            total1 = stat.tile([P, 2], F32, tag="total1")
-            for k in range(2):
-                i = 2 * j + k
-                a = a_ps.tile([P, D], F32, tag="a")
-                nc.tensor.matmul_mx(
-                    out=a[:],
-                    lhsT=sctx_codes[:, i * P : (i + 1) * P].bitcast(FP8X4),
-                    lhsT_scale=sctx_scales[:, i * P : (i + 1) * P],
-                    rhs=wo_codes[:].bitcast(FP8X4),
-                    rhs_scale=wo_scales[:],
-                    start=True,
-                    stop=True,
-                )
-                nc.vector.scalar_tensor_tensor(
-                    out=v1[:, k, :], in0=a[:], scalar=1.0, in1=xb_out[:, i, :], op0=MULT, op1=ADD,
-                    accum_out=total1[:, k : k + 1],
-                )
-            state["w1"], state["std1"] = centre(v1, total1, G_SP)
-
-        def part_b(j):
-            rstd1 = stat.tile([P, 2], F32, tag="rstd1")
-            nc.vector.reciprocal(out=rstd1[:], in_=state["std1"][:])
-            v2 = work.tile([P, 2, D], F32, tag="v2")
-            total2 = stat.tile([P, 2], F32, tag="total2")
-            for k in range(2):
-                nc.vector.scalar_tensor_tensor(
-                    out=v2[:, k, :], in0=state["w1"][:, k, :], scalar=rstd1[:, k : k + 1], in1=xb_sp[:, 2 * j + k, :],
-                    op0=MULT, op1=ADD, accum_out=total2[:, k : k + 1],
-                )
-            state["w2"], state["std2"] = centre(v2, total2, G_2)
-
-        def part_c(j):
-            rstd2 = stat.tile([P, 2], F32, tag="rstd2")
-            nc.vector.reciprocal(out=rstd2[:], in_=state["std2"][:])
-            x2 = work.tile([P, 2, D], F32, tag="x2")
-            x2_grouped = work.tile([P, 2, P, 4], BF16, tag="x2_grouped", align_bytes=64)
-            for k in range(2):
-                nc.vector.scalar_tensor_tensor(
-                    out=x2[:, k, :], in0=state["w2"][:, k, :], scalar=rstd2[:, k : k + 1], in1=ln_bc[:, B_2, :],
-                    op0=MULT, op1=ADD,
-                )
-            nc.sync.dma_start(out=x2_v[:, 2 * j : 2 * j + 2, :], in_=x2[:])
-            for k in range(2):
-                columns = x2[:, k, :].rearrange("p (u c e) -> p u e c", u=2, e=2)
-                turned = turn_ps.tile([P, 4, P], F32, tag="turned")
-                for u in range(2):
-                    for e in range(2):
-                        nc.tensor.transpose(turned[:, 2 * u + e, :], columns[:, u, e, :], ident[:])
-                nc.scalar.copy(out=x2_grouped[:, k, :, :], in_=turned[:].rearrange("p t c -> p c t"))
-            state["x2_grouped"] = x2_grouped
-
-        def part_d(j):
-            x2_codes = work.tile([P, 2 * P], U32, tag="x2_codes", align_bytes=64)
-            x2_scales = work.tile([P, 2 * P], U8, tag="x2_scales", align_bytes=64)
-            nc.vector.quantize_mx(
-                out=x2_codes[:].bitcast(FP8X4),
-                scales=x2_scales[:],
-                in_=state["x2_grouped"][:].rearrange("p k c t -> p (k c t)"),
-            )
-            state["x2_codes", j] = x2_codes
-            state["x2_scales", j] = x2_scales
-
-        def mlp_quarter(j, q):
-            k, half = q // 2, q % 2
-            h_sb = hout.tile([P, 2, BANK], F32, tag="h_sb")
-            for b in range(2):
-                c = 2 * half + b
-                acc = acc_ps.tile([P, BANK], F32, tag="acc")
+            def start_bank(n):
+                i, c = n // F_BANKS, n % F_BANKS
+                half, k = i // HALF, i % HALF
+                acc = psum.tile([P, BANK], F32, tag="bank")
                 nc.tensor.matmul_mx(
                     out=acc[:],
-                    lhsT=state["x2_codes", j][:, k * P : (k + 1) * P].bitcast(FP8X4),
-                    lhsT_scale=state["x2_scales", j][:, k * P : (k + 1) * P],
-                    rhs=w1_codes[:, c * BANK : (c + 1) * BANK].bitcast(FP8X4),
-                    rhs_scale=w1_scales[:, c * BANK : (c + 1) * BANK],
+                    lhsT=live["x2_codes", half][:, k * P : (k + 1) * P].bitcast(FP8X4),
+                    lhsT_scale=live["x2_scales", half][:, k * P : (k + 1) * P],
+                    rhs=fc1_codes[:, c * BANK : (c + 1) * BANK].bitcast(FP8X4),
+                    rhs_scale=fc1_scales[:, c * BANK : (c + 1) * BANK],
                     start=True,
                     stop=True,
                 )
-                nc.vector.tensor_tensor(out=h_sb[:, b, :], in0=acc[:], in1=fc1b_bc[:, c * BANK : (c + 1) * BANK], op=ADD)
-            nc.scalar.activation(out=h_sb[:], in_=h_sb[:], func=ACT.Relu)
-            nc.sync.dma_start(
-                out=h_v[:, 2 * j + k, 2 * half * BANK : 2 * (half + 1) * BANK],
-                in_=h_sb[:].rearrange("p b n -> p (b n)"),
-            )
+                live["acc", n] = acc
 
-        def filler(j, q):
-            if j == 0:
-                prepare_fc1_bank(q)
-                if q > 0:
-                    prepare_sctx_pair(q)
-            else:
-                mlp_quarter(j - 1, q)
+            def finish_bank(n):
+                i, c = n // F_BANKS, n % F_BANKS
+                if n % 2 == 0:
+                    h_sb = hout.tile([P, 2, BANK], F32, tag="h_sb")
+                    live["h_sb"] = h_sb
+                h_sb = live["h_sb"]
+                nc.vector.tensor_tensor(
+                    out=h_sb[:, n % 2, :], in0=live["acc", n][:], in1=fc1b_bc[:, c * BANK : (c + 1) * BANK], op=ADD
+                )
+                if n % 2 == 1:
+                    nc.scalar.activation(out=h_sb[:], in_=h_sb[:], func=ACT.Relu)
+                    nc.sync.dma_start(
+                        out=h_v[:, i, (c - 1) * BANK : (c + 1) * BANK], in_=h_sb[:].rearrange("p b n -> p (b n)")
+                    )
 
-        for j in range(PAIRS + 1):
-            if j < PAIRS:
-                part_a(j)
-            if j == 0:
+            turn_sctx_pair(0)
+            quantise_sctx_pair(0)
+            broadcast_row(B_OUT)
+            for i in range(2):
+                nc.vector.tensor_tensor(out=xb_out[:, i, :], in0=x_sb[:, i, :], in1=ln_bc[:, B_OUT, :], op=ADD)
+            turn_two_row_tiles(wo_sb, 0, wo_grouped)
+            turn_two_row_tiles(wo_sb, 2, wo_grouped)
+            quantise(wo_grouped, wo_codes, wo_scales, 0, D)
+            turn_sctx_pair(1)
+            quantise_sctx_pair(1)
+            broadcast_row(G_SP)
+            broadcast_row(B_SP)
+            for i in range(2, HALF):
+                nc.gpsimd.tensor_tensor(out=xb_out[:, i, :], in0=x_sb[:, i, :], in1=ln_bc[:, B_OUT, :], op=ADD)
+            for i in range(HALF):
+                nc.gpsimd.tensor_tensor(out=xb_sp[:, i, :], in0=x_sb[:, i, :], in1=ln_bc[:, B_SP, :], op=ADD)
+            for i in range(HALF, TILES):
+                nc.gpsimd.tensor_tensor(out=xb_out[:, i, :], in0=x_sb[:, i, :], in1=ln_bc[:, B_OUT, :], op=ADD)
+            for i in range(HALF, TILES):
+                nc.gpsimd.tensor_tensor(out=xb_sp[:, i, :], in0=x_sb[:, i, :], in1=ln_bc[:, B_SP, :], op=ADD)
+
+            def spare_1_of_first_half():
                 broadcast_row(G_2)
                 broadcast_row(B_2)
-            filler(j, 0)
-            if j < PAIRS:
-                part_b(j)
-            filler(j, 1)
-            if j < PAIRS:
-                part_c(j)
-            filler(j, 2)
-            filler(j, 3)
-            if j < PAIRS:
-                part_d(j)
+                turn_sctx_pair(2)
+
+            def spare_2_of_first_half():
+                turn_sctx_pair(3)
+                turn_fc1_half_bank(0)
+                turn_fc1_half_bank(1)
+
+            x2_grouped_0 = layer_norms(0, spare_1_of_first_half, spare_2_of_first_half)
+            turn_fc1_half_bank(2)
+            turn_fc1_half_bank(3)
+            quantise_sctx_pair(2)
+            quantise_sctx_pair(3)
+
+            def spare_1_of_second_half():
+                turn_fc1_half_bank(4)
+                turn_fc1_half_bank(5)
+
+            def spare_2_of_second_half():
+                turn_fc1_half_bank(6)
+                turn_fc1_half_bank(7)
+
+            x2_grouped_1 = layer_norms(1, spare_1_of_second_half, spare_2_of_second_half)
+
+            quantise_x2(0, x2_grouped_0)
+            for c in range(F_BANKS):
+                quantise_fc1_bank(c)
+                if c < AHEAD:
+                    start_bank(c)
+            quantise_x2(1, x2_grouped_1)
+        with tc.tile_pool(name="hout", bufs=H_BUFS, reuse_waits="tile") as hout:
+            for n in range(H_BANKS):
+                finish_bank(n)
+                if n + AHEAD < H_BANKS:
+                    start_bank(n + AHEAD)

@@ -45,7 +45,8 @@ def tile_mlcablock_pb_kernel(
     with ExitStack() as ctx:
         ctx.enter_context(tc.manual_schedule())
         keep = ctx.enter_context(tc.tile_pool(name="keep", bufs=1))
-        psum = ctx.enter_context(tc.psum_pool(name="psum", bufs=8))
+        rows_ps = ctx.enter_context(tc.psum_pool(name="rows_ps", bufs=1))
+        psum = ctx.enter_context(tc.psum_pool(name="psum", bufs=5))
         fc1_codes = keep.tile([P, F], U32, align_bytes=64)
         fc1_scales = keep.tile([P, F], U8, align_bytes=64)
         fc1b_bc = keep.tile([P, F], BF16)
@@ -89,7 +90,8 @@ def tile_mlcablock_pb_kernel(
                 nc.sync.dma_start(out=fc1_sb[:, 4 * c : 4 * c + 4, :], in_=fc1_v[:, 4 * c : 4 * c + 4, :])
             nc.sync.dma_start(out=fc1b_bc[:], in_=fc1_b.partition_broadcast(P))
 
-            ln_bc = prep.tile([P, 5, D], F32)
+            b_out_bc = prep.tile([P, D], F32)
+            b_sp_bc = prep.tile([P, D], F32)
             xb_out = prep.tile([P, TILES, D], F32)
             xb_sp = prep.tile([P, TILES, D], F32)
             wo_grouped = prep.tile([P, D * 4], BF16, align_bytes=64)
@@ -100,12 +102,20 @@ def tile_mlcablock_pb_kernel(
             sctx_scales = prep.tile([P, TOKENS], U8, align_bytes=64)
             fc1_grouped = prep.tile([P, F * 4], BF16, align_bytes=64)
 
-            def broadcast_row(n):
-                spread = psum.tile([P, BANK], F32, tag="bank")
+            def spread_row(n, bank):
                 nc.tensor.matmul(
-                    out=spread[:], lhsT=ident_bf[:, n : n + 1].to_broadcast([P, P]), rhs=ln_rows[:], start=True, stop=True
+                    out=bank[:], lhsT=ident_bf[:, n : n + 1].to_broadcast([P, P]), rhs=ln_rows[:], start=True, stop=True
                 )
-                nc.scalar.copy(out=ln_bc[:, n, :], in_=spread[:])
+
+            def spread_row_to_sbuf(n, dest):
+                bank = psum.tile([P, BANK], F32, tag="bank")
+                spread_row(n, bank)
+                nc.scalar.copy(out=dest, in_=bank[:])
+
+            def spread_row_in_psum(n):
+                bank = rows_ps.tile([P, BANK], F32, name="row_%d" % n)
+                spread_row(n, bank)
+                live["row", n] = bank
 
             def turn_two_row_tiles(rows_sb, r0, grouped):
                 turned = psum.tile([P, 2, 2, P], F32, tag="bank")
@@ -186,7 +196,7 @@ def tile_mlcablock_pb_kernel(
             def centre_and_gain(norm, v, gain, w):
                 for k in range(HALF):
                     nc.vector.scalar_tensor_tensor(
-                        out=w[:, k, :], in0=v[:, k, :], scalar=norm["neg_mean"][:, k : k + 1], in1=ln_bc[:, gain, :],
+                        out=w[:, k, :], in0=v[:, k, :], scalar=norm["neg_mean"][:, k : k + 1], in1=live["row", gain][:],
                         op0=ADD, op1=MULT,
                     )
 
@@ -203,7 +213,7 @@ def tile_mlcablock_pb_kernel(
                 pair_reciprocal(norm2, m)
                 for k in (2 * m, 2 * m + 1):
                     nc.vector.scalar_tensor_tensor(
-                        out=x2[:, k, :], in0=w2[:, k, :], scalar=norm2["rstd"][:, k : k + 1], in1=ln_bc[:, B_2, :],
+                        out=x2[:, k, :], in0=w2[:, k, :], scalar=norm2["rstd"][:, k : k + 1], in1=live["row", B_2][:],
                         op0=MULT, op1=ADD,
                     )
                 first = HALF * half + 2 * m
@@ -276,28 +286,28 @@ def tile_mlcablock_pb_kernel(
 
             turn_sctx_pair(0)
             quantise_sctx_pair(0)
-            broadcast_row(B_OUT)
+            spread_row_to_sbuf(B_OUT, b_out_bc[:])
             for i in range(2):
-                nc.vector.tensor_tensor(out=xb_out[:, i, :], in0=x_sb[:, i, :], in1=ln_bc[:, B_OUT, :], op=ADD)
+                nc.vector.tensor_tensor(out=xb_out[:, i, :], in0=x_sb[:, i, :], in1=b_out_bc[:], op=ADD)
             turn_two_row_tiles(wo_sb, 0, wo_grouped)
             turn_two_row_tiles(wo_sb, 2, wo_grouped)
             quantise(wo_grouped, wo_codes, wo_scales, 0, D)
             turn_sctx_pair(1)
             quantise_sctx_pair(1)
-            broadcast_row(G_SP)
-            broadcast_row(B_SP)
+            spread_row_in_psum(G_SP)
+            spread_row_to_sbuf(B_SP, b_sp_bc[:])
             for i in range(2, HALF):
-                nc.gpsimd.tensor_tensor(out=xb_out[:, i, :], in0=x_sb[:, i, :], in1=ln_bc[:, B_OUT, :], op=ADD)
+                nc.gpsimd.tensor_tensor(out=xb_out[:, i, :], in0=x_sb[:, i, :], in1=b_out_bc[:], op=ADD)
             for i in range(HALF):
-                nc.gpsimd.tensor_tensor(out=xb_sp[:, i, :], in0=x_sb[:, i, :], in1=ln_bc[:, B_SP, :], op=ADD)
+                nc.gpsimd.tensor_tensor(out=xb_sp[:, i, :], in0=x_sb[:, i, :], in1=b_sp_bc[:], op=ADD)
             for i in range(HALF, TILES):
-                nc.gpsimd.tensor_tensor(out=xb_out[:, i, :], in0=x_sb[:, i, :], in1=ln_bc[:, B_OUT, :], op=ADD)
+                nc.gpsimd.tensor_tensor(out=xb_out[:, i, :], in0=x_sb[:, i, :], in1=b_out_bc[:], op=ADD)
             for i in range(HALF, TILES):
-                nc.gpsimd.tensor_tensor(out=xb_sp[:, i, :], in0=x_sb[:, i, :], in1=ln_bc[:, B_SP, :], op=ADD)
+                nc.gpsimd.tensor_tensor(out=xb_sp[:, i, :], in0=x_sb[:, i, :], in1=b_sp_bc[:], op=ADD)
 
             def spare_1_of_first_half():
-                broadcast_row(G_2)
-                broadcast_row(B_2)
+                spread_row_in_psum(G_2)
+                spread_row_in_psum(B_2)
                 turn_sctx_pair(2)
 
             def spare_2_of_first_half():

@@ -18,9 +18,10 @@ F = 2048
 TOKENS = 1024
 EPS = 1e-5
 TILES = TOKENS // P
-HALF = TILES // 2
+PAIRS = TILES // 2
 BANK = 512
 F_BANKS = F // BANK
+PAIR_BANKS = 2 * F_BANKS
 H_BANKS = TILES * F_BANKS
 AHEAD = 3
 H_BUFS = 10
@@ -44,31 +45,120 @@ def tile_mlcablock_pb_kernel(
 
     with ExitStack() as ctx:
         ctx.enter_context(tc.manual_schedule())
+        psum = ctx.enter_context(tc.psum_pool(name="psum", bufs=8))
         keep = ctx.enter_context(tc.tile_pool(name="keep", bufs=1))
-        rows_ps = ctx.enter_context(tc.psum_pool(name="rows_ps", bufs=1))
-        psum = ctx.enter_context(tc.psum_pool(name="psum", bufs=5))
+        late = ctx.enter_context(tc.tile_pool(name="late", bufs=2))
+
         fc1_codes = keep.tile([P, F], U32, align_bytes=64)
         fc1_scales = keep.tile([P, F], U8, align_bytes=64)
         fc1b_bc = keep.tile([P, F], BF16)
+        rows_bc = keep.tile([P, 5, D], F32)
+        ident = keep.tile([P, P], F32)
+        eps = keep.tile([P, 1], F32)
+        x2_codes = {}
+        x2_scales = {}
+        v2_of = {}
+        x2_of = {}
+        norm1 = {}
+        norm2 = {}
+        for j in range(PAIRS):
+            x2_codes[j] = keep.tile([P, 2 * P], U32, name="x2_codes_%d" % j, align_bytes=64)
+            x2_scales[j] = keep.tile([P, 2 * P], U8, name="x2_scales_%d" % j, align_bytes=64)
+            v2_of[j] = keep.tile([P, 2, D], F32, name="v2_%d" % j)
+            x2_of[j] = keep.tile([P, 2, D], F32, name="x2_%d" % j)
+            for norm, which in ((norm1, 1), (norm2, 2)):
+                norm[j] = {}
+                for what in ("total", "neg_mean", "sum_sq", "rstd"):
+                    norm[j][what] = keep.tile([P, 2], F32, name="%s_%d_%d" % (what, which, j))
         live = {}
-        for half in range(2):
-            live["x2_codes", half] = keep.tile([P, HALF * P], U32, name="x2_codes_%d" % half, align_bytes=64)
-            live["x2_scales", half] = keep.tile([P, HALF * P], U8, name="x2_scales_%d" % half, align_bytes=64)
+
+        def both(row):
+            return rows_bc[:, row, :].unsqueeze(1).to_broadcast([P, 2, D])
+
+        def finish_on_vector(j):
+            centred = late.tile([P, 2, D], F32, tag="centred", bufs=1)
+            x2 = x2_of[j]
+            for k in range(2):
+                nc.vector.scalar_tensor_tensor(
+                    out=centred[:, k, :], in0=v2_of[j][:, k, :], scalar=norm2[j]["neg_mean"][:, k : k + 1],
+                    in1=rows_bc[:, G_2, :], op0=ADD, op1=MULT,
+                )
+            for k in range(2):
+                nc.vector.scalar_tensor_tensor(
+                    out=x2[:, k, :], in0=centred[:, k, :], scalar=norm2[j]["rstd"][:, k : k + 1],
+                    in1=rows_bc[:, B_2, :], op0=MULT, op1=ADD,
+                )
+
+        def finish_on_gpsimd(j):
+            x2 = x2_of[j]
+            for k in range(2):
+                nc.gpsimd.tensor_scalar(
+                    out=x2[:, k, :], in0=v2_of[j][:, k, :], scalar1=norm2[j]["neg_mean"][:, k : k + 1],
+                    scalar2=norm2[j]["rstd"][:, k : k + 1], op0=ADD, op1=MULT,
+                )
+            nc.gpsimd.tensor_tensor(out=x2[:], in0=x2[:], in1=both(G_2), op=MULT)
+            nc.gpsimd.tensor_tensor(out=x2[:], in0=x2[:], in1=both(B_2), op=ADD)
+
+        def turn_x2(j):
+            x2 = x2_of[j]
+            nc.sync.dma_start(out=x2_v[:, 2 * j : 2 * j + 2, :], in_=x2[:])
+            x2_grouped = late.tile([P, 2, P, 4], BF16, tag="x2_grouped", align_bytes=64)
+            for k in range(2):
+                columns = x2[:, k, :].rearrange("p (u c e) -> p u e c", u=2, e=2)
+                turned = psum.tile([P, 4, P], F32, tag="bank")
+                for u in range(2):
+                    for e in range(2):
+                        nc.tensor.transpose(turned[:, 2 * u + e, :], columns[:, u, e, :], ident[:])
+                nc.scalar.copy(out=x2_grouped[:, k, :, :], in_=turned[:].rearrange("p t c -> p c t"))
+            live["x2_grouped", j] = x2_grouped
+
+        def quantise_x2(j):
+            nc.vector.quantize_mx(
+                out=x2_codes[j][:].bitcast(FP8X4),
+                scales=x2_scales[j][:],
+                in_=live["x2_grouped", j][:].rearrange("p k c t -> p (k c t)"),
+            )
+
+        def start_bank(n):
+            i, c = n // F_BANKS, n % F_BANKS
+            j, k = i // 2, i % 2
+            acc = psum.tile([P, BANK], F32, tag="bank")
+            nc.tensor.matmul_mx(
+                out=acc[:],
+                lhsT=x2_codes[j][:, k * P : (k + 1) * P].bitcast(FP8X4),
+                lhsT_scale=x2_scales[j][:, k * P : (k + 1) * P],
+                rhs=fc1_codes[:, c * BANK : (c + 1) * BANK].bitcast(FP8X4),
+                rhs_scale=fc1_scales[:, c * BANK : (c + 1) * BANK],
+                start=True,
+                stop=True,
+            )
+            live["acc", n] = acc
+
+        def finish_bank(hout, n):
+            i, c = n // F_BANKS, n % F_BANKS
+            if n % 2 == 0:
+                h_sb = hout.tile([P, 2, BANK], F32, tag="h_sb")
+                live["h_sb"] = h_sb
+            h_sb = live["h_sb"]
+            nc.vector.tensor_tensor(
+                out=h_sb[:, n % 2, :], in0=live["acc", n][:], in1=fc1b_bc[:, c * BANK : (c + 1) * BANK], op=ADD
+            )
+            if n % 2 == 1:
+                nc.scalar.activation(out=h_sb[:], in_=h_sb[:], func=ACT.Relu)
+                nc.sync.dma_start(
+                    out=h_v[:, i, (c - 1) * BANK : (c + 1) * BANK], in_=h_sb[:].rearrange("p b n -> p (b n)")
+                )
 
         with ExitStack() as early:
             prep = early.enter_context(tc.tile_pool(name="prep", bufs=1))
-            work = early.enter_context(tc.tile_pool(name="work", bufs=1))
-            turn = early.enter_context(tc.tile_pool(name="turn", bufs=2))
-            stat = early.enter_context(tc.tile_pool(name="stat", bufs=2))
+            work = early.enter_context(tc.tile_pool(name="work", bufs=2))
             junk = early.enter_context(tc.tile_pool(name="junk", bufs=4))
 
             ln_rows = prep.tile([P, D], BF16)
             nc.vector.memset(ln_rows[:], 0.0)
-            eps = prep.tile([P, 1], F32)
             nc.vector.memset(eps[:], EPS)
             warm = prep.tile([P, 1], F32)
-            nc.scalar.activation(out=warm[:], in_=eps[:], func=ACT.Sqrt)
-            ident = prep.tile([P, P], F32)
+            nc.scalar.activation(out=warm[:], in_=eps[:], func=ACT.Abs_reciprocal_sqrt)
             make_identity(nc, ident[:])
             ident_bf = prep.tile([P, P], BF16)
             make_identity(nc, ident_bf[:])
@@ -82,16 +172,14 @@ def tile_mlcablock_pb_kernel(
             for n, vec in enumerate((out_proj_b, lnsp_g, lnsp_b, ln2_g, ln2_b)):
                 nc.sync.dma_start(out=ln_rows[n : n + 1, :], in_=vec.rearrange("(o d) -> o d", o=1))
             nc.sync.dma_start(out=x_sb[:, 0:2, :], in_=x_v[:, 0:2, :])
-            nc.sync.dma_start(out=sctx_sb[:, 2:HALF, :], in_=sctx_v[:, 2:HALF, :])
-            nc.sync.dma_start(out=x_sb[:, 2:HALF, :], in_=x_v[:, 2:HALF, :])
-            nc.sync.dma_start(out=sctx_sb[:, HALF:TILES, :], in_=sctx_v[:, HALF:TILES, :])
-            nc.sync.dma_start(out=x_sb[:, HALF:TILES, :], in_=x_v[:, HALF:TILES, :])
+            nc.sync.dma_start(out=sctx_sb[:, 2:4, :], in_=sctx_v[:, 2:4, :])
+            nc.sync.dma_start(out=x_sb[:, 2:4, :], in_=x_v[:, 2:4, :])
+            nc.sync.dma_start(out=sctx_sb[:, 4:TILES, :], in_=sctx_v[:, 4:TILES, :])
+            nc.sync.dma_start(out=x_sb[:, 4:TILES, :], in_=x_v[:, 4:TILES, :])
             for c in range(F_BANKS):
                 nc.sync.dma_start(out=fc1_sb[:, 4 * c : 4 * c + 4, :], in_=fc1_v[:, 4 * c : 4 * c + 4, :])
             nc.sync.dma_start(out=fc1b_bc[:], in_=fc1_b.partition_broadcast(P))
 
-            b_out_bc = prep.tile([P, D], F32)
-            b_sp_bc = prep.tile([P, D], F32)
             xb_out = prep.tile([P, TILES, D], F32)
             xb_sp = prep.tile([P, TILES, D], F32)
             wo_grouped = prep.tile([P, D * 4], BF16, align_bytes=64)
@@ -102,20 +190,13 @@ def tile_mlcablock_pb_kernel(
             sctx_scales = prep.tile([P, TOKENS], U8, align_bytes=64)
             fc1_grouped = prep.tile([P, F * 4], BF16, align_bytes=64)
 
-            def spread_row(n, bank):
+            def spread_row(n):
+                spread = psum.tile([P, BANK], F32, tag="bank")
                 nc.tensor.matmul(
-                    out=bank[:], lhsT=ident_bf[:, n : n + 1].to_broadcast([P, P]), rhs=ln_rows[:], start=True, stop=True
+                    out=spread[:], lhsT=ident_bf[:, n : n + 1].to_broadcast([P, P]), rhs=ln_rows[:],
+                    start=True, stop=True,
                 )
-
-            def spread_row_to_sbuf(n, dest):
-                bank = psum.tile([P, BANK], F32, tag="bank")
-                spread_row(n, bank)
-                nc.scalar.copy(out=dest, in_=bank[:])
-
-            def spread_row_in_psum(n):
-                bank = rows_ps.tile([P, BANK], F32, name="row_%d" % n)
-                spread_row(n, bank)
-                live["row", n] = bank
+                nc.scalar.copy(out=rows_bc[:, n, :], in_=spread[:])
 
             def turn_two_row_tiles(rows_sb, r0, grouped):
                 turned = psum.tile([P, 2, 2, P], F32, tag="bank")
@@ -124,7 +205,9 @@ def tile_mlcablock_pb_kernel(
                     for u in range(2):
                         nc.tensor.transpose(turned[:, r, u, :], words[:, u * P : (u + 1) * P], ident[:])
                 nc.scalar.copy(
-                    out=grouped[:, r0 * P * 4 : (r0 + 2) * P * 4].bitcast(F32).rearrange("p (r c u) -> p r c u", r=2, u=2),
+                    out=grouped[:, r0 * P * 4 : (r0 + 2) * P * 4]
+                    .bitcast(F32)
+                    .rearrange("p (r c u) -> p r c u", r=2, u=2),
                     in_=turned[:].rearrange("p r u c -> p r c u"),
                 )
 
@@ -144,39 +227,28 @@ def tile_mlcablock_pb_kernel(
             def turn_fc1_half_bank(b):
                 turn_two_row_tiles(fc1_sb, 2 * b, fc1_grouped)
 
-            def quantise_fc1_bank(c):
-                quantise(fc1_grouped, fc1_codes, fc1_scales, c * BANK, BANK)
+            def add_bias(engine, xb, row, j):
+                pair = slice(2 * j, 2 * j + 2)
+                engine.tensor_tensor(out=xb[:, pair, :], in0=x_sb[:, pair, :], in1=both(row), op=ADD)
 
-            def open_norm():
-                total = stat.tile([P, HALF], F32, tag="total")
-                neg_mean = stat.tile([P, HALF], F32, tag="neg_mean")
-                sum_sq = stat.tile([P, HALF], F32, tag="sum_sq")
-                std = stat.tile([P, HALF], F32, tag="std")
-                rstd = stat.tile([P, HALF], F32, tag="rstd")
-                return {"total": total, "neg_mean": neg_mean, "sum_sq": sum_sq, "std": std, "rstd": rstd}
-
-            def pair_statistics(norm, v, m):
-                pair = slice(2 * m, 2 * m + 2)
+            def statistics(norm, v):
                 nc.vector.tensor_scalar(
-                    out=norm["neg_mean"][:, pair], in0=norm["total"][:, pair], scalar1=-1.0 / D, scalar2=None, op0=MULT
+                    out=norm["neg_mean"][:], in0=norm["total"][:], scalar1=-1.0 / D, scalar2=None, op0=MULT
                 )
-                for k in (2 * m, 2 * m + 1):
+                for k in range(2):
                     squares = junk.tile([P, D], BF16, tag="squares")
                     nc.scalar.activation(
-                        out=squares[:], in_=v[:, k, :], func=ACT.Square, bias=norm["neg_mean"][:, k : k + 1], scale=1.0,
-                        accum_out=norm["sum_sq"][:, k : k + 1],
+                        out=squares[:], in_=v[:, k, :], func=ACT.Square, bias=norm["neg_mean"][:, k : k + 1],
+                        scale=1.0, accum_out=norm["sum_sq"][:, k : k + 1],
                     )
                 nc.scalar.activation(
-                    out=norm["std"][:, pair], in_=norm["sum_sq"][:, pair], func=ACT.Sqrt, bias=eps[:], scale=1.0 / D
+                    out=norm["rstd"][:], in_=norm["sum_sq"][:], func=ACT.Abs_reciprocal_sqrt, bias=eps[:], scale=1.0 / D
                 )
 
-            def pair_reciprocal(norm, m):
-                pair = slice(2 * m, 2 * m + 2)
-                nc.vector.reciprocal(out=norm["rstd"][:, pair], in_=norm["std"][:, pair])
-
-            def first_residual(half, norm, v1, m):
-                for k in (2 * m, 2 * m + 1):
-                    i = HALF * half + k
+            def first_residual(j):
+                v1 = work.tile([P, 2, D], F32, tag="v1")
+                for k in range(2):
+                    i = 2 * j + k
                     a = psum.tile([P, D], F32, tag="bank")
                     nc.tensor.matmul_mx(
                         out=a[:],
@@ -189,156 +261,92 @@ def tile_mlcablock_pb_kernel(
                     )
                     nc.vector.scalar_tensor_tensor(
                         out=v1[:, k, :], in0=a[:], scalar=1.0, in1=xb_out[:, i, :], op0=MULT, op1=ADD,
-                        accum_out=norm["total"][:, k : k + 1],
+                        accum_out=norm1[j]["total"][:, k : k + 1],
                     )
-                pair_statistics(norm, v1, m)
+                statistics(norm1[j], v1)
+                live["v1", j] = v1
 
-            def centre_and_gain(norm, v, gain, w):
-                for k in range(HALF):
+            def centre_and_gain(j):
+                centred = work.tile([P, 2, D], F32, tag="centred")
+                for k in range(2):
                     nc.vector.scalar_tensor_tensor(
-                        out=w[:, k, :], in0=v[:, k, :], scalar=norm["neg_mean"][:, k : k + 1], in1=live["row", gain][:],
-                        op0=ADD, op1=MULT,
+                        out=centred[:, k, :], in0=live["v1", j][:, k, :], scalar=norm1[j]["neg_mean"][:, k : k + 1],
+                        in1=rows_bc[:, G_SP, :], op0=ADD, op1=MULT,
                     )
+                live["centred", j] = centred
 
-            def second_residual(half, norm1, w1, norm2, v2, m):
-                pair_reciprocal(norm1, m)
-                for k in (2 * m, 2 * m + 1):
+            def second_residual(j):
+                for k in range(2):
                     nc.vector.scalar_tensor_tensor(
-                        out=v2[:, k, :], in0=w1[:, k, :], scalar=norm1["rstd"][:, k : k + 1],
-                        in1=xb_sp[:, HALF * half + k, :], op0=MULT, op1=ADD, accum_out=norm2["total"][:, k : k + 1],
+                        out=v2_of[j][:, k, :], in0=live["centred", j][:, k, :], scalar=norm1[j]["rstd"][:, k : k + 1],
+                        in1=xb_sp[:, 2 * j + k, :], op0=MULT, op1=ADD, accum_out=norm2[j]["total"][:, k : k + 1],
                     )
-                pair_statistics(norm2, v2, m)
-
-            def finish_x2(half, norm2, w2, x2, x2_grouped, m):
-                pair_reciprocal(norm2, m)
-                for k in (2 * m, 2 * m + 1):
-                    nc.vector.scalar_tensor_tensor(
-                        out=x2[:, k, :], in0=w2[:, k, :], scalar=norm2["rstd"][:, k : k + 1], in1=live["row", B_2][:],
-                        op0=MULT, op1=ADD,
-                    )
-                first = HALF * half + 2 * m
-                nc.sync.dma_start(out=x2_v[:, first : first + 2, :], in_=x2[:, 2 * m : 2 * m + 2, :])
-                for k in (2 * m, 2 * m + 1):
-                    columns = x2[:, k, :].rearrange("p (u c e) -> p u e c", u=2, e=2)
-                    turned = psum.tile([P, 4, P], F32, tag="bank")
-                    for u in range(2):
-                        for e in range(2):
-                            nc.tensor.transpose(turned[:, 2 * u + e, :], columns[:, u, e, :], ident[:])
-                    nc.scalar.copy(out=x2_grouped[:, k, :, :], in_=turned[:].rearrange("p t c -> p c t"))
-
-            def layer_norms(half, scalar_spare_1, scalar_spare_2):
-                norm1 = open_norm()
-                norm2 = open_norm()
-                v1 = work.tile([P, HALF, D], F32, tag="v1")
-                w1 = work.tile([P, HALF, D], F32, tag="w")
-                v2 = work.tile([P, HALF, D], F32, tag="v2")
-                x2 = turn.tile([P, HALF, D], F32, tag="x2")
-                x2_grouped = turn.tile([P, HALF, P, 4], BF16, tag="x2_grouped", align_bytes=64)
-                first_residual(half, norm1, v1, 0)
-                first_residual(half, norm1, v1, 1)
-                centre_and_gain(norm1, v1, G_SP, w1)
-                scalar_spare_1()
-                second_residual(half, norm1, w1, norm2, v2, 0)
-                second_residual(half, norm1, w1, norm2, v2, 1)
-                w2 = work.tile([P, HALF, D], F32, tag="w")
-                centre_and_gain(norm2, v2, G_2, w2)
-                scalar_spare_2()
-                finish_x2(half, norm2, w2, x2, x2_grouped, 0)
-                finish_x2(half, norm2, w2, x2, x2_grouped, 1)
-                return x2_grouped
-
-            def quantise_x2(half, x2_grouped):
-                nc.vector.quantize_mx(
-                    out=live["x2_codes", half][:].bitcast(FP8X4),
-                    scales=live["x2_scales", half][:],
-                    in_=x2_grouped[:].rearrange("p k c t -> p (k c t)"),
-                )
-
-            def start_bank(n):
-                i, c = n // F_BANKS, n % F_BANKS
-                half, k = i // HALF, i % HALF
-                acc = psum.tile([P, BANK], F32, tag="bank")
-                nc.tensor.matmul_mx(
-                    out=acc[:],
-                    lhsT=live["x2_codes", half][:, k * P : (k + 1) * P].bitcast(FP8X4),
-                    lhsT_scale=live["x2_scales", half][:, k * P : (k + 1) * P],
-                    rhs=fc1_codes[:, c * BANK : (c + 1) * BANK].bitcast(FP8X4),
-                    rhs_scale=fc1_scales[:, c * BANK : (c + 1) * BANK],
-                    start=True,
-                    stop=True,
-                )
-                live["acc", n] = acc
-
-            def finish_bank(n):
-                i, c = n // F_BANKS, n % F_BANKS
-                if n % 2 == 0:
-                    h_sb = hout.tile([P, 2, BANK], F32, tag="h_sb")
-                    live["h_sb"] = h_sb
-                h_sb = live["h_sb"]
-                nc.vector.tensor_tensor(
-                    out=h_sb[:, n % 2, :], in0=live["acc", n][:], in1=fc1b_bc[:, c * BANK : (c + 1) * BANK], op=ADD
-                )
-                if n % 2 == 1:
-                    nc.scalar.activation(out=h_sb[:], in_=h_sb[:], func=ACT.Relu)
-                    nc.sync.dma_start(
-                        out=h_v[:, i, (c - 1) * BANK : (c + 1) * BANK], in_=h_sb[:].rearrange("p b n -> p (b n)")
-                    )
+                statistics(norm2[j], v2_of[j])
 
             turn_sctx_pair(0)
             quantise_sctx_pair(0)
-            spread_row_to_sbuf(B_OUT, b_out_bc[:])
-            for i in range(2):
-                nc.vector.tensor_tensor(out=xb_out[:, i, :], in0=x_sb[:, i, :], in1=b_out_bc[:], op=ADD)
+            spread_row(B_OUT)
+            add_bias(nc.vector, xb_out, B_OUT, 0)
             turn_two_row_tiles(wo_sb, 0, wo_grouped)
             turn_two_row_tiles(wo_sb, 2, wo_grouped)
             quantise(wo_grouped, wo_codes, wo_scales, 0, D)
             turn_sctx_pair(1)
             quantise_sctx_pair(1)
-            spread_row_in_psum(G_SP)
-            spread_row_to_sbuf(B_SP, b_sp_bc[:])
-            for i in range(2, HALF):
-                nc.gpsimd.tensor_tensor(out=xb_out[:, i, :], in0=x_sb[:, i, :], in1=b_out_bc[:], op=ADD)
-            for i in range(HALF):
-                nc.gpsimd.tensor_tensor(out=xb_sp[:, i, :], in0=x_sb[:, i, :], in1=b_sp_bc[:], op=ADD)
-            for i in range(HALF, TILES):
-                nc.gpsimd.tensor_tensor(out=xb_out[:, i, :], in0=x_sb[:, i, :], in1=b_out_bc[:], op=ADD)
-            for i in range(HALF, TILES):
-                nc.gpsimd.tensor_tensor(out=xb_sp[:, i, :], in0=x_sb[:, i, :], in1=b_sp_bc[:], op=ADD)
+            spread_row(G_SP)
+            spread_row(B_SP)
+            add_bias(nc.gpsimd, xb_out, B_OUT, 1)
+            add_bias(nc.gpsimd, xb_sp, B_SP, 0)
+            add_bias(nc.gpsimd, xb_sp, B_SP, 1)
+            add_bias(nc.gpsimd, xb_out, B_OUT, 2)
+            add_bias(nc.gpsimd, xb_out, B_OUT, 3)
+            add_bias(nc.gpsimd, xb_sp, B_SP, 2)
+            add_bias(nc.gpsimd, xb_sp, B_SP, 3)
 
-            def spare_1_of_first_half():
-                spread_row_in_psum(G_2)
-                spread_row_in_psum(B_2)
-                turn_sctx_pair(2)
-
-            def spare_2_of_first_half():
-                turn_sctx_pair(3)
-                turn_fc1_half_bank(0)
-                turn_fc1_half_bank(1)
-
-            x2_grouped_0 = layer_norms(0, spare_1_of_first_half, spare_2_of_first_half)
-            turn_fc1_half_bank(2)
-            turn_fc1_half_bank(3)
+            first_residual(0)
+            first_residual(1)
+            centre_and_gain(0)
+            centre_and_gain(1)
+            turn_sctx_pair(2)
+            turn_sctx_pair(3)
+            second_residual(0)
+            second_residual(1)
+            spread_row(G_2)
+            spread_row(B_2)
+            turn_fc1_half_bank(0)
+            turn_fc1_half_bank(1)
             quantise_sctx_pair(2)
             quantise_sctx_pair(3)
 
-            def spare_1_of_second_half():
-                turn_fc1_half_bank(4)
-                turn_fc1_half_bank(5)
+            first_residual(2)
+            first_residual(3)
+            for b in range(2, 6):
+                turn_fc1_half_bank(b)
+            finish_on_vector(0)
+            turn_x2(0)
+            finish_on_gpsimd(1)
+            centre_and_gain(2)
+            centre_and_gain(3)
+            second_residual(2)
+            second_residual(3)
+            for b in range(6, 8):
+                turn_fc1_half_bank(b)
 
-            def spare_2_of_second_half():
-                turn_fc1_half_bank(6)
-                turn_fc1_half_bank(7)
-
-            x2_grouped_1 = layer_norms(1, spare_1_of_second_half, spare_2_of_second_half)
-
-            quantise_x2(0, x2_grouped_0)
+            quantise_x2(0)
             for c in range(F_BANKS):
-                quantise_fc1_bank(c)
+                quantise(fc1_grouped, fc1_codes, fc1_scales, c * BANK, BANK)
                 if c < AHEAD:
                     start_bank(c)
-            quantise_x2(1, x2_grouped_1)
+            for j in range(2, PAIRS):
+                finish_on_gpsimd(j)
+
         with tc.tile_pool(name="hout", bufs=H_BUFS, reuse_waits="tile") as hout:
-            for n in range(H_BANKS):
-                finish_bank(n)
-                if n + AHEAD < H_BANKS:
-                    start_bank(n + AHEAD)
+            for j in range(PAIRS):
+                first = j * PAIR_BANKS
+                if j + 1 < PAIRS:
+                    turn_x2(j + 1)
+                for n in range(first, first + PAIR_BANKS):
+                    if n + AHEAD == first + PAIR_BANKS and j + 1 < PAIRS:
+                        quantise_x2(j + 1)
+                    finish_bank(hout, n)
+                    if n + AHEAD < H_BANKS:
+                        start_bank(n + AHEAD)

@@ -89,16 +89,6 @@ def tile_mlcablock_pb_kernel(
                     in1=rows_bc[:, B_2, :], op0=MULT, op1=ADD,
                 )
 
-        def finish_on_gpsimd(j):
-            x2 = x2_of[j]
-            for k in range(2):
-                nc.gpsimd.tensor_scalar(
-                    out=x2[:, k, :], in0=v2_of[j][:, k, :], scalar1=norm2[j]["neg_mean"][:, k : k + 1],
-                    scalar2=norm2[j]["rstd"][:, k : k + 1], op0=ADD, op1=MULT,
-                )
-            nc.gpsimd.tensor_tensor(out=x2[:], in0=x2[:], in1=both(G_2), op=MULT)
-            nc.gpsimd.tensor_tensor(out=x2[:], in0=x2[:], in1=both(B_2), op=ADD)
-
         def turn_x2(j):
             x2 = x2_of[j]
             nc.sync.dma_start(out=x2_v[:, 2 * j : 2 * j + 2, :], in_=x2[:])
@@ -323,7 +313,7 @@ def tile_mlcablock_pb_kernel(
                 turn_fc1_half_bank(b)
             finish_on_vector(0)
             turn_x2(0)
-            finish_on_gpsimd(1)
+            finish_on_vector(1)
             centre_and_gain(2)
             centre_and_gain(3)
             second_residual(2)
@@ -336,8 +326,6 @@ def tile_mlcablock_pb_kernel(
                 quantise(fc1_grouped, fc1_codes, fc1_scales, c * BANK, BANK)
                 if c < AHEAD:
                     start_bank(c)
-            for j in range(2, PAIRS):
-                finish_on_gpsimd(j)
 
         with tc.tile_pool(name="hout", bufs=H_BUFS, reuse_waits="tile") as hout:
             for j in range(PAIRS):
@@ -350,3 +338,5 @@ def tile_mlcablock_pb_kernel(
                     finish_bank(hout, n)
                     if n + AHEAD < H_BANKS:
                         start_bank(n + AHEAD)
+                if j + 2 < PAIRS:
+                    finish_on_vector(j + 2)

@@ -28,7 +28,7 @@ H_BUFS = 10
 
 FLOPS = 2 * TOKENS * D * (D + F)
 
-B_OUT, G_SP, B_SP, G_2, B_2 = 0, 1, 2, 3, 4
+B_OUT, G_SP, B_SP = 0, 1, 2
 
 
 def tile_mlcablock_pb_kernel(
@@ -52,7 +52,9 @@ def tile_mlcablock_pb_kernel(
         fc1_codes = keep.tile([P, F], U32, align_bytes=64)
         fc1_scales = keep.tile([P, F], U8, align_bytes=64)
         fc1b_bc = keep.tile([P, F], BF16)
-        rows_bc = keep.tile([P, 5, D], F32)
+        rows_bc = keep.tile([P, 3, D], F32)
+        g2_bc = keep.tile([P, D], BF16)
+        b2_bc = keep.tile([P, D], BF16)
         ident = keep.tile([P, P], F32)
         eps = keep.tile([P, 1], F32)
         x2_codes = {}
@@ -81,12 +83,12 @@ def tile_mlcablock_pb_kernel(
             for k in range(2):
                 nc.vector.scalar_tensor_tensor(
                     out=centred[:, k, :], in0=v2_of[j][:, k, :], scalar=norm2[j]["neg_mean"][:, k : k + 1],
-                    in1=rows_bc[:, G_2, :], op0=ADD, op1=MULT,
+                    in1=g2_bc[:], op0=ADD, op1=MULT,
                 )
             for k in range(2):
                 nc.vector.scalar_tensor_tensor(
                     out=x2[:, k, :], in0=centred[:, k, :], scalar=norm2[j]["rstd"][:, k : k + 1],
-                    in1=rows_bc[:, B_2, :], op0=MULT, op1=ADD,
+                    in1=b2_bc[:], op0=MULT, op1=ADD,
                 )
 
         def turn_x2(j):
@@ -159,19 +161,20 @@ def tile_mlcablock_pb_kernel(
             fc1_sb = prep.tile([P, F // P, D], BF16)
             nc.sync.dma_start(out=sctx_sb[:, 0:2, :], in_=sctx_v[:, 0:2, :])
             nc.sync.dma_start(out=wo_sb[:], in_=wo_v)
-            for n, vec in enumerate((out_proj_b, lnsp_g, lnsp_b, ln2_g, ln2_b)):
+            for n, vec in enumerate((out_proj_b, lnsp_g, lnsp_b)):
                 nc.sync.dma_start(out=ln_rows[n : n + 1, :], in_=vec.rearrange("(o d) -> o d", o=1))
-            nc.sync.dma_start(out=x_sb[:, 0:2, :], in_=x_v[:, 0:2, :])
+            nc.sync.dma_start(out=x_sb[:, 0:4, :], in_=x_v[:, 0:4, :])
             nc.sync.dma_start(out=sctx_sb[:, 2:4, :], in_=sctx_v[:, 2:4, :])
-            nc.sync.dma_start(out=x_sb[:, 2:4, :], in_=x_v[:, 2:4, :])
             nc.sync.dma_start(out=sctx_sb[:, 4:TILES, :], in_=sctx_v[:, 4:TILES, :])
             nc.sync.dma_start(out=x_sb[:, 4:TILES, :], in_=x_v[:, 4:TILES, :])
             for c in range(F_BANKS):
                 nc.sync.dma_start(out=fc1_sb[:, 4 * c : 4 * c + 4, :], in_=fc1_v[:, 4 * c : 4 * c + 4, :])
+            nc.sync.dma_start(out=g2_bc[:], in_=ln2_g.partition_broadcast(P))
+            nc.sync.dma_start(out=b2_bc[:], in_=ln2_b.partition_broadcast(P))
             nc.sync.dma_start(out=fc1b_bc[:], in_=fc1_b.partition_broadcast(P))
 
             xb_out = prep.tile([P, TILES, D], F32)
-            xb_sp = prep.tile([P, TILES, D], F32)
+            xb_sp0 = prep.tile([P, 2, D], F32)
             wo_grouped = prep.tile([P, D * 4], BF16, align_bytes=64)
             wo_codes = prep.tile([P, D], U32, align_bytes=64)
             wo_scales = prep.tile([P, D], U8, align_bytes=64)
@@ -217,9 +220,19 @@ def tile_mlcablock_pb_kernel(
             def turn_fc1_half_bank(b):
                 turn_two_row_tiles(fc1_sb, 2 * b, fc1_grouped)
 
-            def add_bias(engine, xb, row, j):
+            def add_bias(xb, row, j):
                 pair = slice(2 * j, 2 * j + 2)
-                engine.tensor_tensor(out=xb[:, pair, :], in0=x_sb[:, pair, :], in1=both(row), op=ADD)
+                nc.vector.tensor_tensor(out=xb[:, pair, :], in0=x_sb[:, pair, :], in1=both(row), op=ADD)
+
+            def add_bias_in_psum(j):
+                for k in range(2):
+                    xb = psum.tile([P, D], F32, tag="bank")
+                    nc.tensor.matmul(out=xb[:], lhsT=ident_bf[:], rhs=x_sb[:, 2 * j + k, :], start=True, stop=False)
+                    nc.tensor.matmul(
+                        out=xb[:], lhsT=ident_bf[:, B_SP : B_SP + 1].to_broadcast([P, P]), rhs=ln_rows[:],
+                        start=False, stop=True,
+                    )
+                    live["xb_sp", j, k] = xb[:]
 
             def statistics(norm, v):
                 nc.vector.tensor_scalar(
@@ -269,14 +282,15 @@ def tile_mlcablock_pb_kernel(
                 for k in range(2):
                     nc.vector.scalar_tensor_tensor(
                         out=v2_of[j][:, k, :], in0=live["centred", j][:, k, :], scalar=norm1[j]["rstd"][:, k : k + 1],
-                        in1=xb_sp[:, 2 * j + k, :], op0=MULT, op1=ADD, accum_out=norm2[j]["total"][:, k : k + 1],
+                        in1=live["xb_sp", j, k], op0=MULT, op1=ADD, accum_out=norm2[j]["total"][:, k : k + 1],
                     )
                 statistics(norm2[j], v2_of[j])
 
             turn_sctx_pair(0)
             quantise_sctx_pair(0)
             spread_row(B_OUT)
-            add_bias(nc.vector, xb_out, B_OUT, 0)
+            add_bias(xb_out, B_OUT, 0)
+            add_bias(xb_out, B_OUT, 1)
             turn_two_row_tiles(wo_sb, 0, wo_grouped)
             turn_two_row_tiles(wo_sb, 2, wo_grouped)
             quantise(wo_grouped, wo_codes, wo_scales, 0, D)
@@ -284,24 +298,21 @@ def tile_mlcablock_pb_kernel(
             quantise_sctx_pair(1)
             spread_row(G_SP)
             spread_row(B_SP)
-            add_bias(nc.gpsimd, xb_out, B_OUT, 1)
-            add_bias(nc.gpsimd, xb_sp, B_SP, 0)
-            add_bias(nc.gpsimd, xb_sp, B_SP, 1)
-            add_bias(nc.gpsimd, xb_out, B_OUT, 2)
-            add_bias(nc.gpsimd, xb_out, B_OUT, 3)
-            add_bias(nc.gpsimd, xb_sp, B_SP, 2)
-            add_bias(nc.gpsimd, xb_sp, B_SP, 3)
+            nc.vector.tensor_tensor(out=xb_sp0[:], in0=x_sb[:, 0:2, :], in1=both(B_SP), op=ADD)
+            for k in range(2):
+                live["xb_sp", 0, k] = xb_sp0[:, k, :]
 
             first_residual(0)
             first_residual(1)
             centre_and_gain(0)
             centre_and_gain(1)
+            add_bias(xb_out, B_OUT, 2)
             turn_sctx_pair(2)
             turn_sctx_pair(3)
+            add_bias_in_psum(1)
             second_residual(0)
             second_residual(1)
-            spread_row(G_2)
-            spread_row(B_2)
+            add_bias(xb_out, B_OUT, 3)
             turn_fc1_half_bank(0)
             turn_fc1_half_bank(1)
             quantise_sctx_pair(2)
@@ -316,7 +327,9 @@ def tile_mlcablock_pb_kernel(
             finish_on_vector(1)
             centre_and_gain(2)
             centre_and_gain(3)
+            add_bias_in_psum(2)
             second_residual(2)
+            add_bias_in_psum(3)
             second_residual(3)
             for b in range(6, 8):
                 turn_fc1_half_bank(b)

@@ -10,6 +10,7 @@ U8 = mybir.dt.uint8
 FP8X4 = mybir.dt.float8_e4m3fn_x4
 ADD = mybir.AluOpType.add
 MULT = mybir.AluOpType.mult
+MAX = mybir.AluOpType.max
 ACT = mybir.ActivationFunctionType
 
 P = 128
@@ -21,14 +22,16 @@ TILES = TOKENS // P
 PAIRS = TILES // 2
 BANK = 512
 F_BANKS = F // BANK
-PAIR_BANKS = 2 * F_BANKS
-H_BANKS = TILES * F_BANKS
-AHEAD = 3
+TURNED = {0: (2, 3), 1: (3,), 2: (), 3: ()}
+BANKS = 8
+ACC_BUFS = 3
+AHEAD = ACC_BUFS
 H_BUFS = 10
 
 FLOPS = 2 * TOKENS * D * (D + F)
 
-B_OUT, G_SP, B_SP = 0, 1, 2
+B_OUT, G_SP, B_SP, B_FC1 = 0, 1, 2, 3
+VECTORS = 5
 
 
 def tile_mlcablock_pb_kernel(
@@ -52,7 +55,9 @@ def tile_mlcablock_pb_kernel(
         fc1_codes = keep.tile([P, F], U32, align_bytes=64)
         fc1_scales = keep.tile([P, F], U8, align_bytes=64)
         fc1b_bc = keep.tile([P, F], BF16)
-        rows_bc = keep.tile([P, 3, D], F32)
+        fc1b_col = keep.tile([P, F_BANKS, 2], F32)
+        bo_bc = keep.tile([P, D], BF16)
+        g_bc = keep.tile([P, D], BF16)
         g2_bc = keep.tile([P, D], BF16)
         b2_bc = keep.tile([P, D], BF16)
         ident = keep.tile([P, P], F32)
@@ -74,9 +79,6 @@ def tile_mlcablock_pb_kernel(
                     norm[j][what] = keep.tile([P, 2], F32, name="%s_%d_%d" % (what, which, j))
         live = {}
 
-        def both(row):
-            return rows_bc[:, row, :].unsqueeze(1).to_broadcast([P, 2, D])
-
         def finish_on_vector(j):
             centred = late.tile([P, 2, D], F32, tag="centred", bufs=1)
             x2 = x2_of[j]
@@ -97,7 +99,7 @@ def tile_mlcablock_pb_kernel(
             x2_grouped = late.tile([P, 2, P, 4], BF16, tag="x2_grouped", align_bytes=64)
             for k in range(2):
                 columns = x2[:, k, :].rearrange("p (u c e) -> p u e c", u=2, e=2)
-                turned = psum.tile([P, 4, P], F32, tag="bank")
+                turned = psum.tile([P, 4, P], F32, tag="bank", bufs=BANKS - ACC_BUFS)
                 for u in range(2):
                     for e in range(2):
                         nc.tensor.transpose(turned[:, 2 * u + e, :], columns[:, u, e, :], ident[:])
@@ -111,37 +113,107 @@ def tile_mlcablock_pb_kernel(
                 in_=live["x2_grouped", j][:].rearrange("p k c t -> p (k c t)"),
             )
 
-        def start_bank(n):
-            i, c = n // F_BANKS, n % F_BANKS
-            j, k = i // 2, i % 2
-            acc = psum.tile([P, BANK], F32, tag="bank")
-            nc.tensor.matmul_mx(
-                out=acc[:],
-                lhsT=x2_codes[j][:, k * P : (k + 1) * P].bitcast(FP8X4),
-                lhsT_scale=x2_scales[j][:, k * P : (k + 1) * P],
-                rhs=fc1_codes[:, c * BANK : (c + 1) * BANK].bitcast(FP8X4),
-                rhs_scale=fc1_scales[:, c * BANK : (c + 1) * BANK],
-                start=True,
-                stop=True,
-            )
-            live["acc", n] = acc
+        banks = []
+        banks_up_to = {}
+        for j in range(PAIRS):
+            straight = [c for c in range(F_BANKS) if c not in TURNED[j]]
+            banks += [(j, k, c) for k in range(2) for c in straight[0:2]]
+            if len(straight) == 3:
+                banks += [(j, k, straight[2]) for k in range(2)]
+            elif len(straight) == 4:
+                banks += [(j, k, c) for k in range(2) for c in straight[2:4]]
+            banks_up_to[j] = len(banks)
+        progress = {"started": 0, "finished": 0, "allowed": 0}
 
-        def finish_bank(hout, n):
-            i, c = n // F_BANKS, n % F_BANKS
-            if n % 2 == 0:
-                h_sb = hout.tile([P, 2, BANK], F32, tag="h_sb")
-                live["h_sb"] = h_sb
-            h_sb = live["h_sb"]
-            nc.vector.tensor_tensor(
-                out=h_sb[:, n % 2, :], in0=live["acc", n][:], in1=fc1b_bc[:, c * BANK : (c + 1) * BANK], op=ADD
-            )
-            if n % 2 == 1:
-                nc.scalar.activation(out=h_sb[:], in_=h_sb[:], func=ACT.Relu)
-                nc.sync.dma_start(
-                    out=h_v[:, i, (c - 1) * BANK : (c + 1) * BANK], in_=h_sb[:].rearrange("p b n -> p (b n)")
+        def start_banks(upto):
+            while progress["started"] < min(upto, progress["allowed"], len(banks)):
+                n = progress["started"]
+                j, k, c = banks[n]
+                acc = psum.tile([P, BANK], F32, tag="acc", bufs=ACC_BUFS)
+                nc.tensor.matmul_mx(
+                    out=acc[:],
+                    lhsT=x2_codes[j][:, k * P : (k + 1) * P].bitcast(FP8X4),
+                    lhsT_scale=x2_scales[j][:, k * P : (k + 1) * P],
+                    rhs=fc1_codes[:, c * BANK : (c + 1) * BANK].bitcast(FP8X4),
+                    rhs_scale=fc1_scales[:, c * BANK : (c + 1) * BANK],
+                    start=True,
+                    stop=True,
                 )
+                live["acc", n] = acc
+                progress["started"] = n + 1
+
+        def two_banks(relu_engine):
+            n = progress["finished"]
+            h_sb = hout.tile([P, 2, BANK], F32, tag="h_sb")
+            for e in range(2):
+                c = banks[n + e][2]
+                nc.vector.tensor_tensor(
+                    out=h_sb[:, e, :], in0=live["acc", n + e][:], in1=fc1b_bc[:, c * BANK : (c + 1) * BANK], op=ADD
+                )
+                start_banks(n + e + 1 + AHEAD)
+            if relu_engine == "scalar":
+                nc.scalar.activation(out=h_sb[:], in_=h_sb[:], func=ACT.Relu)
+            else:
+                nc.vector.tensor_scalar(out=h_sb[:], in0=h_sb[:], scalar1=0.0, scalar2=None, op0=MAX)
+            j, k, c = banks[n]
+            if banks[n + 1][1] != k:
+                nc.sync.dma_start(out=h_v[:, 2 * j : 2 * j + 2, c * BANK : (c + 1) * BANK], in_=h_sb[:])
+            else:
+                nc.sync.dma_start(
+                    out=h_v[:, 2 * j + k, c * BANK : (c + 2) * BANK], in_=h_sb[:].rearrange("p b n -> p (b n)")
+                )
+            progress["finished"] = n + 2
+
+        def last_two_banks():
+            n = progress["finished"]
+            h_sb = hout.tile([P, 2, BANK], F32, tag="h_sb")
+            for e in range(2):
+                j, k, c = banks[n + e]
+                nc.vector.tensor_tensor(
+                    out=h_sb[:, e, :], in0=live["acc", n + e][:], in1=fc1b_bc[:, c * BANK : (c + 1) * BANK], op=ADD
+                )
+                if e == 0:
+                    nc.scalar.activation(out=h_sb[:, e, :], in_=h_sb[:, e, :], func=ACT.Relu)
+                else:
+                    nc.vector.tensor_scalar(
+                        out=h_sb[:, e, :], in0=h_sb[:, e, :], scalar1=0.0, scalar2=None, op0=MAX
+                    )
+                nc.sync.dma_start(out=h_v[:, 2 * j + k, c * BANK : (c + 1) * BANK], in_=h_sb[:, e, :])
+
+        def start_turned(j, c):
+            h_turned = late.tile([P, F_BANKS, 2 * P], F32, tag="h_turned")
+            for half in range(2):
+                acc = psum.tile([P, 2, 2 * P], F32, tag="bank", bufs=BANKS - ACC_BUFS)
+                for e in range(2):
+                    first = c * BANK + (2 * half + e) * P
+                    nc.tensor.matmul_mx(
+                        out=acc[:, e, :],
+                        lhsT=fc1_codes[:, first : first + P].bitcast(FP8X4),
+                        lhsT_scale=fc1_scales[:, first : first + P],
+                        rhs=x2_codes[j][:].bitcast(FP8X4),
+                        rhs_scale=x2_scales[j][:],
+                        start=True,
+                        stop=True,
+                    )
+                for e in range(2):
+                    r = 2 * half + e
+                    nc.scalar.activation(
+                        out=h_turned[:, r, :], in_=acc[:, e, :], func=ACT.Relu, bias=fc1b_col[:, r, c - 2 : c - 1],
+                        scale=1.0,
+                    )
+            live["h_turned", j, c] = h_turned
+
+        def finish_turned(j, c):
+            h_sb = hout.tile([P, 2, BANK], F32, tag="h_sb")
+            for k in range(2):
+                back = psum.tile([P, F_BANKS, P], F32, tag="bank", bufs=BANKS - ACC_BUFS)
+                for r in range(F_BANKS):
+                    nc.tensor.transpose(back[:, r, :], live["h_turned", j, c][:, r, k * P : (k + 1) * P], ident[:])
+                nc.scalar.copy(out=h_sb[:, k, :], in_=back[:].rearrange("p r c -> p (r c)"))
+            nc.sync.dma_start(out=h_v[:, 2 * j : 2 * j + 2, c * BANK : (c + 1) * BANK], in_=h_sb[:])
 
         with ExitStack() as early:
+            hout = early.enter_context(tc.tile_pool(name="hout", bufs=H_BUFS, reuse_waits="tile"))
             prep = early.enter_context(tc.tile_pool(name="prep", bufs=1))
             work = early.enter_context(tc.tile_pool(name="work", bufs=2))
             junk = early.enter_context(tc.tile_pool(name="junk", bufs=4))
@@ -159,22 +231,29 @@ def tile_mlcablock_pb_kernel(
             sctx_sb = prep.tile([P, TILES, D], BF16)
             x_sb = prep.tile([P, TILES, D], BF16)
             fc1_sb = prep.tile([P, F // P, D], BF16)
+            def load_fc1(c):
+                nc.sync.dma_start(out=fc1_sb[:, 4 * c : 4 * c + 4, :], in_=fc1_v[:, 4 * c : 4 * c + 4, :])
+
             nc.sync.dma_start(out=sctx_sb[:, 0:2, :], in_=sctx_v[:, 0:2, :])
-            nc.sync.dma_start(out=wo_sb[:], in_=wo_v)
             for n, vec in enumerate((out_proj_b, lnsp_g, lnsp_b)):
                 nc.sync.dma_start(out=ln_rows[n : n + 1, :], in_=vec.rearrange("(o d) -> o d", o=1))
-            nc.sync.dma_start(out=x_sb[:, 0:4, :], in_=x_v[:, 0:4, :])
+            nc.sync.dma_start(out=ln_rows[B_FC1 : B_FC1 + 2, :], in_=fc1_b[2 * BANK : F].rearrange("(o d) -> o d", o=2))
+            nc.sync.dma_start(out=x_sb[:, 0:2, :], in_=x_v[:, 0:2, :])
+            nc.sync.dma_start(out=wo_sb[:], in_=wo_v)
             nc.sync.dma_start(out=sctx_sb[:, 2:4, :], in_=sctx_v[:, 2:4, :])
-            nc.sync.dma_start(out=sctx_sb[:, 4:TILES, :], in_=sctx_v[:, 4:TILES, :])
+            nc.sync.dma_start(out=x_sb[:, 2:4, :], in_=x_v[:, 2:4, :])
+            load_fc1(0)
+            load_fc1(1)
             nc.sync.dma_start(out=x_sb[:, 4:TILES, :], in_=x_v[:, 4:TILES, :])
-            for c in range(F_BANKS):
-                nc.sync.dma_start(out=fc1_sb[:, 4 * c : 4 * c + 4, :], in_=fc1_v[:, 4 * c : 4 * c + 4, :])
+            load_fc1(2)
+            load_fc1(3)
+            nc.sync.dma_start(out=sctx_sb[:, 4:TILES, :], in_=sctx_v[:, 4:TILES, :])
             nc.sync.dma_start(out=g2_bc[:], in_=ln2_g.partition_broadcast(P))
             nc.sync.dma_start(out=b2_bc[:], in_=ln2_b.partition_broadcast(P))
             nc.sync.dma_start(out=fc1b_bc[:], in_=fc1_b.partition_broadcast(P))
 
             xb_out = prep.tile([P, TILES, D], F32)
-            xb_sp0 = prep.tile([P, 2, D], F32)
+            vec_cols = prep.tile([P, F_BANKS, VECTORS], BF16)
             wo_grouped = prep.tile([P, D * 4], BF16, align_bytes=64)
             wo_codes = prep.tile([P, D], U32, align_bytes=64)
             wo_scales = prep.tile([P, D], U8, align_bytes=64)
@@ -183,16 +262,22 @@ def tile_mlcablock_pb_kernel(
             sctx_scales = prep.tile([P, TOKENS], U8, align_bytes=64)
             fc1_grouped = prep.tile([P, F * 4], BF16, align_bytes=64)
 
-            def spread_row(n):
-                spread = psum.tile([P, BANK], F32, tag="bank")
-                nc.tensor.matmul(
-                    out=spread[:], lhsT=ident_bf[:, n : n + 1].to_broadcast([P, P]), rhs=ln_rows[:],
-                    start=True, stop=True,
-                )
-                nc.scalar.copy(out=rows_bc[:, n, :], in_=spread[:])
+            def turn_vectors():
+                turned = psum.tile([P, F_BANKS, P], BF16, tag="bank", bufs=BANKS - ACC_BUFS)
+                for r in range(F_BANKS):
+                    nc.tensor.transpose(turned[:, r, :], ln_rows[:, r * P : (r + 1) * P], ident_bf[:])
+                nc.scalar.copy(out=vec_cols[:], in_=turned[:, :, 0:VECTORS])
+
+            def spread_row(n, tag, bufs):
+                spread = psum.tile([P, D], BF16, tag=tag, bufs=bufs)
+                for r in range(F_BANKS):
+                    nc.tensor.transpose(
+                        spread[:, r * P : (r + 1) * P], vec_cols[:, r, n : n + 1].to_broadcast([P, P]), ident_bf[:]
+                    )
+                return spread
 
             def turn_two_row_tiles(rows_sb, r0, grouped):
-                turned = psum.tile([P, 2, 2, P], F32, tag="bank")
+                turned = psum.tile([P, 2, 2, P], F32, tag="bank", bufs=BANKS - ACC_BUFS)
                 for r in range(2):
                     words = rows_sb[:, r0 + r, :].bitcast(F32)
                     for u in range(2):
@@ -220,13 +305,13 @@ def tile_mlcablock_pb_kernel(
             def turn_fc1_half_bank(b):
                 turn_two_row_tiles(fc1_sb, 2 * b, fc1_grouped)
 
-            def add_bias(xb, row, j):
-                pair = slice(2 * j, 2 * j + 2)
-                nc.vector.tensor_tensor(out=xb[:, pair, :], in0=x_sb[:, pair, :], in1=both(row), op=ADD)
+            def add_out_bias(engine, j, k, bias):
+                i = 2 * j + k
+                engine.tensor_tensor(out=xb_out[:, i, :], in0=x_sb[:, i, :], in1=bias, op=ADD)
 
             def add_bias_in_psum(j):
                 for k in range(2):
-                    xb = psum.tile([P, D], F32, tag="bank")
+                    xb = psum.tile([P, D], F32, tag="bank", bufs=BANKS - ACC_BUFS)
                     nc.tensor.matmul(out=xb[:], lhsT=ident_bf[:], rhs=x_sb[:, 2 * j + k, :], start=True, stop=False)
                     nc.tensor.matmul(
                         out=xb[:], lhsT=ident_bf[:, B_SP : B_SP + 1].to_broadcast([P, P]), rhs=ln_rows[:],
@@ -235,9 +320,7 @@ def tile_mlcablock_pb_kernel(
                     live["xb_sp", j, k] = xb[:]
 
             def statistics(norm, v):
-                nc.vector.tensor_scalar(
-                    out=norm["neg_mean"][:], in0=norm["total"][:], scalar1=-1.0 / D, scalar2=None, op0=MULT
-                )
+                nc.scalar.mul(norm["neg_mean"][:], norm["total"][:], -1.0 / D)
                 for k in range(2):
                     squares = junk.tile([P, D], BF16, tag="squares")
                     nc.scalar.activation(
@@ -248,11 +331,10 @@ def tile_mlcablock_pb_kernel(
                     out=norm["rstd"][:], in_=norm["sum_sq"][:], func=ACT.Abs_reciprocal_sqrt, bias=eps[:], scale=1.0 / D
                 )
 
-            def first_residual(j):
-                v1 = work.tile([P, 2, D], F32, tag="v1")
+            def project(j):
                 for k in range(2):
                     i = 2 * j + k
-                    a = psum.tile([P, D], F32, tag="bank")
+                    a = psum.tile([P, D], F32, tag="bank", bufs=BANKS - ACC_BUFS)
                     nc.tensor.matmul_mx(
                         out=a[:],
                         lhsT=sctx_codes[:, i * P : (i + 1) * P].bitcast(FP8X4),
@@ -262,19 +344,24 @@ def tile_mlcablock_pb_kernel(
                         start=True,
                         stop=True,
                     )
+                    live["a", j, k] = a
+
+            def first_residual(j):
+                v1 = work.tile([P, 2, D], F32, tag="v1")
+                for k in range(2):
                     nc.vector.scalar_tensor_tensor(
-                        out=v1[:, k, :], in0=a[:], scalar=1.0, in1=xb_out[:, i, :], op0=MULT, op1=ADD,
+                        out=v1[:, k, :], in0=live["a", j, k][:], scalar=1.0, in1=xb_out[:, 2 * j + k, :], op0=MULT, op1=ADD,
                         accum_out=norm1[j]["total"][:, k : k + 1],
                     )
                 statistics(norm1[j], v1)
                 live["v1", j] = v1
 
-            def centre_and_gain(j):
+            def centre_and_gain(j, gain):
                 centred = work.tile([P, 2, D], F32, tag="centred")
                 for k in range(2):
                     nc.vector.scalar_tensor_tensor(
                         out=centred[:, k, :], in0=live["v1", j][:, k, :], scalar=norm1[j]["neg_mean"][:, k : k + 1],
-                        in1=rows_bc[:, G_SP, :], op0=ADD, op1=MULT,
+                        in1=gain[:], op0=ADD, op1=MULT,
                     )
                 live["centred", j] = centred
 
@@ -288,68 +375,98 @@ def tile_mlcablock_pb_kernel(
 
             turn_sctx_pair(0)
             quantise_sctx_pair(0)
-            spread_row(B_OUT)
-            add_bias(xb_out, B_OUT, 0)
-            add_bias(xb_out, B_OUT, 1)
+            turn_vectors()
+            bo_psum = spread_row(B_OUT, "bank", BANKS - ACC_BUFS)
+            for k in range(2):
+                add_out_bias(nc.vector, 0, k, bo_psum[:])
             turn_two_row_tiles(wo_sb, 0, wo_grouped)
             turn_two_row_tiles(wo_sb, 2, wo_grouped)
             quantise(wo_grouped, wo_codes, wo_scales, 0, D)
+            nc.scalar.copy(out=bo_bc[:], in_=bo_psum[:])
+            for j in range(1, PAIRS):
+                for k in range(2):
+                    add_out_bias(nc.gpsimd, j, k, bo_bc[:])
             turn_sctx_pair(1)
-            quantise_sctx_pair(1)
-            spread_row(G_SP)
-            spread_row(B_SP)
-            nc.vector.tensor_tensor(out=xb_sp0[:], in0=x_sb[:, 0:2, :], in1=both(B_SP), op=ADD)
-            for k in range(2):
-                live["xb_sp", 0, k] = xb_sp0[:, k, :]
+            g_psum = spread_row(G_SP, "acc", ACC_BUFS)
+            nc.scalar.copy(out=g_bc[:], in_=g_psum[:])
+            nc.scalar.copy(out=fc1b_col[:], in_=vec_cols[:, :, B_FC1 : B_FC1 + 2])
 
-            first_residual(0)
-            first_residual(1)
-            centre_and_gain(0)
-            centre_and_gain(1)
-            add_bias(xb_out, B_OUT, 2)
-            turn_sctx_pair(2)
-            turn_sctx_pair(3)
-            add_bias_in_psum(1)
-            second_residual(0)
-            second_residual(1)
-            add_bias(xb_out, B_OUT, 3)
+            def fc1_bank(c):
+                quantise(fc1_grouped, fc1_codes, fc1_scales, c * BANK, BANK)
+
+            def pair_is_quantised(j):
+                progress["allowed"] = banks_up_to[j]
+                start_banks(progress["finished"] + AHEAD)
+
+            project(0)
             turn_fc1_half_bank(0)
             turn_fc1_half_bank(1)
-            quantise_sctx_pair(2)
-            quantise_sctx_pair(3)
-
-            first_residual(2)
-            first_residual(3)
-            for b in range(2, 6):
-                turn_fc1_half_bank(b)
+            first_residual(0)
+            quantise_sctx_pair(1)
+            project(1)
+            turn_fc1_half_bank(2)
+            centre_and_gain(0, g_psum)
+            first_residual(1)
+            add_bias_in_psum(0)
+            turn_fc1_half_bank(3)
+            turn_fc1_half_bank(4)
+            second_residual(0)
+            centre_and_gain(1, g_psum)
+            turn_fc1_half_bank(5)
+            turn_fc1_half_bank(6)
+            turn_fc1_half_bank(7)
+            fc1_bank(0)
+            add_bias_in_psum(1)
             finish_on_vector(0)
             turn_x2(0)
+            second_residual(1)
+            fc1_bank(2)
+            fc1_bank(3)
+            quantise_x2(0)
+            start_turned(0, 2)
+            fc1_bank(1)
+            pair_is_quantised(0)
+            turn_sctx_pair(2)
+            turn_sctx_pair(3)
             finish_on_vector(1)
-            centre_and_gain(2)
-            centre_and_gain(3)
+            quantise_sctx_pair(2)
+            finish_turned(0, 2)
+            turn_x2(1)
+            two_banks("scalar")
+            project(2)
+            quantise_sctx_pair(3)
+            first_residual(2)
+            quantise_x2(1)
+            project(3)
+            two_banks("scalar")
+            pair_is_quantised(1)
+            start_turned(0, 3)
+            first_residual(3)
+            centre_and_gain(2, g_bc)
             add_bias_in_psum(2)
+            finish_turned(0, 3)
+            two_banks("scalar")
             second_residual(2)
             add_bias_in_psum(3)
+            centre_and_gain(3, g_bc)
+            start_turned(1, 3)
+            two_banks("scalar")
             second_residual(3)
-            for b in range(6, 8):
-                turn_fc1_half_bank(b)
-
-            quantise_x2(0)
-            for c in range(F_BANKS):
-                quantise(fc1_grouped, fc1_codes, fc1_scales, c * BANK, BANK)
-                if c < AHEAD:
-                    start_bank(c)
-
-        with tc.tile_pool(name="hout", bufs=H_BUFS, reuse_waits="tile") as hout:
-            for j in range(PAIRS):
-                first = j * PAIR_BANKS
-                if j + 1 < PAIRS:
-                    turn_x2(j + 1)
-                for n in range(first, first + PAIR_BANKS):
-                    if n + AHEAD == first + PAIR_BANKS and j + 1 < PAIRS:
-                        quantise_x2(j + 1)
-                    finish_bank(hout, n)
-                    if n + AHEAD < H_BANKS:
-                        start_bank(n + AHEAD)
-                if j + 2 < PAIRS:
-                    finish_on_vector(j + 2)
+            finish_on_vector(2)
+            turn_x2(2)
+            finish_turned(1, 3)
+            finish_on_vector(3)
+            quantise_x2(2)
+            two_banks("scalar")
+            pair_is_quantised(2)
+            turn_x2(3)
+            two_banks("scalar")
+            two_banks("scalar")
+            quantise_x2(3)
+            pair_is_quantised(3)
+            two_banks("scalar")
+            two_banks("scalar")
+            two_banks("scalar")
+            two_banks("scalar")
+            two_banks("scalar")
+            last_two_banks()

@@ -93,24 +93,25 @@ def tile_mlcablock_pb_kernel(
                     in1=b2_bc[:], op0=MULT, op1=ADD,
                 )
 
-        def turn_x2(j):
-            x2 = x2_of[j]
-            nc.sync.dma_start(out=x2_v[:, 2 * j : 2 * j + 2, :], in_=x2[:])
-            x2_grouped = late.tile([P, 2, P, 4], BF16, tag="x2_grouped", align_bytes=64)
+        def round_x2(j, engine):
+            nc.sync.dma_start(out=x2_v[:, 2 * j : 2 * j + 2, :], in_=x2_of[j][:])
+            x2_bf = late.tile([P, 2, D], BF16, tag="x2_bf")
             for k in range(2):
-                columns = x2[:, k, :].rearrange("p (u c e) -> p u e c", u=2, e=2)
-                turned = psum.tile([P, 4, P], F32, tag="bank", bufs=BANKS - ACC_BUFS)
-                for u in range(2):
-                    for e in range(2):
-                        nc.tensor.transpose(turned[:, 2 * u + e, :], columns[:, u, e, :], ident[:])
-                nc.scalar.copy(out=x2_grouped[:, k, :, :], in_=turned[:].rearrange("p t c -> p c t"))
+                engine.tensor_scalar(
+                    out=x2_bf[:, k, :], in0=x2_of[j][:, k, :], scalar1=1.0, scalar2=0.0, op0=MULT, op1=ADD
+                )
+            live["x2_bf", j] = x2_bf
+
+        def turn_x2(j):
+            x2_grouped = late.tile([P, 2 * P * 4], BF16, tag="x2_grouped", align_bytes=64)
+            turn_two_row_tiles(live["x2_bf", j], 0, x2_grouped)
             live["x2_grouped", j] = x2_grouped
 
         def quantise_x2(j):
             nc.vector.quantize_mx(
                 out=x2_codes[j][:].bitcast(FP8X4),
                 scales=x2_scales[j][:],
-                in_=live["x2_grouped", j][:].rearrange("p k c t -> p (k c t)"),
+                in_=live["x2_grouped", j][:],
             )
 
         banks = []
@@ -143,6 +144,10 @@ def tile_mlcablock_pb_kernel(
                 progress["started"] = n + 1
 
         def two_banks(relu_engine):
+            add_bias_to_two_banks()
+            finish_two_banks(relu_engine)
+
+        def add_bias_to_two_banks():
             n = progress["finished"]
             h_sb = hout.tile([P, 2, BANK], F32, tag="h_sb")
             for e in range(2):
@@ -151,6 +156,12 @@ def tile_mlcablock_pb_kernel(
                     out=h_sb[:, e, :], in0=live["acc", n + e][:], in1=fc1b_bc[:, c * BANK : (c + 1) * BANK], op=ADD
                 )
                 start_banks(n + e + 1 + AHEAD)
+            live["h_sb"] = h_sb
+            progress["finished"] = n + 2
+
+        def finish_two_banks(relu_engine):
+            n = progress["finished"] - 2
+            h_sb = live["h_sb"]
             if relu_engine == "scalar":
                 nc.scalar.activation(out=h_sb[:], in_=h_sb[:], func=ACT.Relu)
             else:
@@ -162,7 +173,6 @@ def tile_mlcablock_pb_kernel(
                 nc.sync.dma_start(
                     out=h_v[:, 2 * j + k, c * BANK : (c + 2) * BANK], in_=h_sb[:].rearrange("p b n -> p (b n)")
                 )
-            progress["finished"] = n + 2
 
         def last_two_banks():
             n = progress["finished"]
@@ -234,12 +244,13 @@ def tile_mlcablock_pb_kernel(
             def load_fc1(c):
                 nc.sync.dma_start(out=fc1_sb[:, 4 * c : 4 * c + 4, :], in_=fc1_v[:, 4 * c : 4 * c + 4, :])
 
+            nc.sync.dma_start(out=wo_sb[:, 0:2, :], in_=wo_v[:, 0:2, :])
+            nc.sync.dma_start(out=wo_sb[:, 2:4, :], in_=wo_v[:, 2:4, :])
             nc.sync.dma_start(out=sctx_sb[:, 0:2, :], in_=sctx_v[:, 0:2, :])
             for n, vec in enumerate((out_proj_b, lnsp_g, lnsp_b)):
                 nc.sync.dma_start(out=ln_rows[n : n + 1, :], in_=vec.rearrange("(o d) -> o d", o=1))
             nc.sync.dma_start(out=ln_rows[B_FC1 : B_FC1 + 2, :], in_=fc1_b[2 * BANK : F].rearrange("(o d) -> o d", o=2))
             nc.sync.dma_start(out=x_sb[:, 0:2, :], in_=x_v[:, 0:2, :])
-            nc.sync.dma_start(out=wo_sb[:], in_=wo_v)
             nc.sync.dma_start(out=sctx_sb[:, 2:4, :], in_=sctx_v[:, 2:4, :])
             nc.sync.dma_start(out=x_sb[:, 2:4, :], in_=x_v[:, 2:4, :])
             load_fc1(0)
@@ -276,13 +287,13 @@ def tile_mlcablock_pb_kernel(
                     )
                 return spread
 
-            def turn_two_row_tiles(rows_sb, r0, grouped):
+            def turn_two_row_tiles(rows_sb, r0, grouped, copy=nc.scalar.copy):
                 turned = psum.tile([P, 2, 2, P], F32, tag="bank", bufs=BANKS - ACC_BUFS)
                 for r in range(2):
                     words = rows_sb[:, r0 + r, :].bitcast(F32)
                     for u in range(2):
                         nc.tensor.transpose(turned[:, r, u, :], words[:, u * P : (u + 1) * P], ident[:])
-                nc.scalar.copy(
+                copy(
                     out=grouped[:, r0 * P * 4 : (r0 + 2) * P * 4]
                     .bitcast(F32)
                     .rearrange("p (r c u) -> p r c u", r=2, u=2),
@@ -309,9 +320,9 @@ def tile_mlcablock_pb_kernel(
                 i = 2 * j + k
                 engine.tensor_tensor(out=xb_out[:, i, :], in0=x_sb[:, i, :], in1=bias, op=ADD)
 
-            def add_bias_in_psum(j):
+            def add_bias_in_psum(j, tag="bank", bufs=BANKS - ACC_BUFS):
                 for k in range(2):
-                    xb = psum.tile([P, D], F32, tag="bank", bufs=BANKS - ACC_BUFS)
+                    xb = psum.tile([P, D], F32, tag=tag, bufs=bufs)
                     nc.tensor.matmul(out=xb[:], lhsT=ident_bf[:], rhs=x_sb[:, 2 * j + k, :], start=True, stop=False)
                     nc.tensor.matmul(
                         out=xb[:], lhsT=ident_bf[:, B_SP : B_SP + 1].to_broadcast([P, P]), rhs=ln_rows[:],
@@ -324,17 +335,17 @@ def tile_mlcablock_pb_kernel(
                 for k in range(2):
                     squares = junk.tile([P, D], BF16, tag="squares")
                     nc.scalar.activation(
-                        out=squares[:], in_=v[:, k, :], func=ACT.Square, bias=norm["neg_mean"][:, k : k + 1],
-                        scale=1.0, accum_out=norm["sum_sq"][:, k : k + 1],
+                        out=squares[:], in_=v[:, k, :], func=ACT.Square, bias=norm["total"][:, k : k + 1],
+                        scale=-1.0 * D, accum_out=norm["sum_sq"][:, k : k + 1],
                     )
                 nc.scalar.activation(
-                    out=norm["rstd"][:], in_=norm["sum_sq"][:], func=ACT.Abs_reciprocal_sqrt, bias=eps[:], scale=1.0 / D
+                    out=norm["rstd"][:], in_=norm["sum_sq"][:], func=ACT.Abs_reciprocal_sqrt, bias=eps[:], scale=1.0 / D**3
                 )
 
-            def project(j):
+            def project(j, tag="bank", bufs=BANKS - ACC_BUFS):
                 for k in range(2):
                     i = 2 * j + k
-                    a = psum.tile([P, D], F32, tag="bank", bufs=BANKS - ACC_BUFS)
+                    a = psum.tile([P, D], F32, tag=tag, bufs=bufs)
                     nc.tensor.matmul_mx(
                         out=a[:],
                         lhsT=sctx_codes[:, i * P : (i + 1) * P].bitcast(FP8X4),
@@ -373,23 +384,27 @@ def tile_mlcablock_pb_kernel(
                     )
                 statistics(norm2[j], v2_of[j])
 
+            turn_two_row_tiles(wo_sb, 0, wo_grouped)
+            turn_two_row_tiles(wo_sb, 2, wo_grouped, nc.vector.tensor_copy)
             turn_sctx_pair(0)
-            quantise_sctx_pair(0)
+            quantise(wo_grouped, wo_codes, wo_scales, 0, D)
             turn_vectors()
             bo_psum = spread_row(B_OUT, "bank", BANKS - ACC_BUFS)
-            for k in range(2):
-                add_out_bias(nc.vector, 0, k, bo_psum[:])
-            turn_two_row_tiles(wo_sb, 0, wo_grouped)
-            turn_two_row_tiles(wo_sb, 2, wo_grouped)
-            quantise(wo_grouped, wo_codes, wo_scales, 0, D)
+            quantise_sctx_pair(0)
             nc.scalar.copy(out=bo_bc[:], in_=bo_psum[:])
-            for j in range(1, PAIRS):
-                for k in range(2):
-                    add_out_bias(nc.gpsimd, j, k, bo_bc[:])
             turn_sctx_pair(1)
-            g_psum = spread_row(G_SP, "acc", ACC_BUFS)
+            g_psum = spread_row(G_SP, "bank", BANKS - ACC_BUFS)
+            project(0, "acc", ACC_BUFS)
             nc.scalar.copy(out=g_bc[:], in_=g_psum[:])
             nc.scalar.copy(out=fc1b_col[:], in_=vec_cols[:, :, B_FC1 : B_FC1 + 2])
+            for k in range(2):
+                add_out_bias(nc.vector, 0, k, bo_psum[:])
+            for k in range(2):
+                add_out_bias(nc.vector, 1, k, bo_bc[:])
+            for j in range(2, PAIRS):
+                for k in range(2):
+                    add_out_bias(nc.gpsimd, j, k, bo_bc[:])
+            quantise_sctx_pair(1)
 
             def fc1_bank(c):
                 quantise(fc1_grouped, fc1_codes, fc1_scales, c * BANK, BANK)
@@ -398,73 +413,76 @@ def tile_mlcablock_pb_kernel(
                 progress["allowed"] = banks_up_to[j]
                 start_banks(progress["finished"] + AHEAD)
 
-            project(0)
             turn_fc1_half_bank(0)
             turn_fc1_half_bank(1)
             first_residual(0)
-            quantise_sctx_pair(1)
             project(1)
-            turn_fc1_half_bank(2)
-            centre_and_gain(0, g_psum)
+            turn_fc1_half_bank(0)
+            turn_fc1_half_bank(1)
+            centre_and_gain(0, g_bc)
+            add_bias_in_psum(0, "acc", ACC_BUFS)
             first_residual(1)
-            add_bias_in_psum(0)
+            turn_fc1_half_bank(2)
             turn_fc1_half_bank(3)
-            turn_fc1_half_bank(4)
             second_residual(0)
-            centre_and_gain(1, g_psum)
-            turn_fc1_half_bank(5)
-            turn_fc1_half_bank(6)
-            turn_fc1_half_bank(7)
+            centre_and_gain(1, g_bc)
+            add_bias_in_psum(1, "acc", ACC_BUFS)
+            for b in range(4, 8):
+                turn_fc1_half_bank(b)
             fc1_bank(0)
-            add_bias_in_psum(1)
             finish_on_vector(0)
+            round_x2(0, nc.gpsimd)
+            turn_sctx_pair(2)
+            turn_sctx_pair(3)
             turn_x2(0)
             second_residual(1)
             fc1_bank(2)
             fc1_bank(3)
             quantise_x2(0)
             start_turned(0, 2)
+            quantise_sctx_pair(2)
             fc1_bank(1)
             pair_is_quantised(0)
-            turn_sctx_pair(2)
-            turn_sctx_pair(3)
-            finish_on_vector(1)
-            quantise_sctx_pair(2)
-            finish_turned(0, 2)
-            turn_x2(1)
-            two_banks("scalar")
-            project(2)
             quantise_sctx_pair(3)
-            first_residual(2)
-            quantise_x2(1)
-            project(3)
+            finish_on_vector(1)
+            round_x2(1, nc.gpsimd)
+            finish_turned(0, 2)
+            project(2)
             two_banks("scalar")
-            pair_is_quantised(1)
-            start_turned(0, 3)
-            first_residual(3)
-            centre_and_gain(2, g_bc)
+            first_residual(2)
+            turn_x2(1)
             add_bias_in_psum(2)
+            two_banks("scalar")
+            start_turned(0, 3)
+            centre_and_gain(2, g_bc)
+            quantise_x2(1)
+            pair_is_quantised(1)
+            second_residual(2)
+            project(3)
+            first_residual(3)
             finish_turned(0, 3)
             two_banks("scalar")
-            second_residual(2)
+            finish_on_vector(2)
+            round_x2(2, nc.gpsimd)
             add_bias_in_psum(3)
-            centre_and_gain(3, g_bc)
             start_turned(1, 3)
             two_banks("scalar")
-            second_residual(3)
-            finish_on_vector(2)
             turn_x2(2)
+            centre_and_gain(3, g_bc)
+            second_residual(3)
             finish_turned(1, 3)
-            finish_on_vector(3)
+            add_bias_to_two_banks()
             quantise_x2(2)
-            two_banks("scalar")
             pair_is_quantised(2)
-            turn_x2(3)
+            finish_two_banks("vector")
+            finish_on_vector(3)
+            round_x2(3, nc.gpsimd)
             two_banks("scalar")
+            two_banks("scalar")
+            turn_x2(3)
             two_banks("scalar")
             quantise_x2(3)
             pair_is_quantised(3)
-            two_banks("scalar")
             two_banks("scalar")
             two_banks("scalar")
             two_banks("scalar")

@@ -96,15 +96,28 @@ def tile_mlcablock_pb_kernel(
         def round_x2(j, engine):
             nc.sync.dma_start(out=x2_v[:, 2 * j : 2 * j + 2, :], in_=x2_of[j][:])
             x2_bf = late.tile([P, 2, D], BF16, tag="x2_bf")
-            for k in range(2):
-                engine.tensor_scalar(
-                    out=x2_bf[:, k, :], in0=x2_of[j][:, k, :], scalar1=1.0, scalar2=0.0, op0=MULT, op1=ADD
-                )
+            engine.tensor_scalar(out=x2_bf[:], in0=x2_of[j][:], scalar1=1.0, scalar2=0.0, op0=MULT, op1=ADD)
             live["x2_bf", j] = x2_bf
 
         def turn_x2(j):
             x2_grouped = late.tile([P, 2 * P * 4], BF16, tag="x2_grouped", align_bytes=64)
             turn_two_row_tiles(live["x2_bf", j], 0, x2_grouped)
+            live["x2_grouped", j] = x2_grouped
+
+        def turn_x2_direct(j):
+            x2 = x2_of[j]
+            nc.sync.dma_start(out=x2_v[:, 2 * j : 2 * j + 2, :], in_=x2[:])
+            x2_grouped = late.tile([P, 2 * P * 4], BF16, tag="x2_grouped", align_bytes=64)
+            for k in range(2):
+                columns = x2[:, k, :].rearrange("p (u c e) -> p u e c", u=2, e=2)
+                turned = psum.tile([P, 4, P], F32, tag="bank", bufs=BANKS - ACC_BUFS)
+                for u in range(2):
+                    for e in range(2):
+                        nc.tensor.transpose(turned[:, 2 * u + e, :], columns[:, u, e, :], ident[:])
+                nc.scalar.copy(
+                    out=x2_grouped[:, k * P * 4 : (k + 1) * P * 4].rearrange("p (c t) -> p c t", t=4),
+                    in_=turned[:].rearrange("p t c -> p c t"),
+                )
             live["x2_grouped", j] = x2_grouped
 
         def quantise_x2(j):
@@ -393,10 +406,8 @@ def tile_mlcablock_pb_kernel(
             quantise_sctx_pair(0)
             nc.scalar.copy(out=bo_bc[:], in_=bo_psum[:])
             turn_sctx_pair(1)
-            g_psum = spread_row(G_SP, "bank", BANKS - ACC_BUFS)
             project(0, "acc", ACC_BUFS)
-            nc.scalar.copy(out=g_bc[:], in_=g_psum[:])
-            nc.scalar.copy(out=fc1b_col[:], in_=vec_cols[:, :, B_FC1 : B_FC1 + 2])
+            g_psum = spread_row(G_SP, "acc", ACC_BUFS)
             for k in range(2):
                 add_out_bias(nc.vector, 0, k, bo_psum[:])
             for k in range(2):
@@ -418,14 +429,16 @@ def tile_mlcablock_pb_kernel(
             first_residual(0)
             project(1)
             turn_fc1_half_bank(0)
+            nc.scalar.copy(out=g_bc[:], in_=g_psum[:])
+            nc.scalar.copy(out=fc1b_col[:], in_=vec_cols[:, :, B_FC1 : B_FC1 + 2])
+            centre_and_gain(0, g_psum)
             turn_fc1_half_bank(1)
-            centre_and_gain(0, g_bc)
             add_bias_in_psum(0, "acc", ACC_BUFS)
             first_residual(1)
             turn_fc1_half_bank(2)
             turn_fc1_half_bank(3)
             second_residual(0)
-            centre_and_gain(1, g_bc)
+            centre_and_gain(1, g_psum)
             add_bias_in_psum(1, "acc", ACC_BUFS)
             for b in range(4, 8):
                 turn_fc1_half_bank(b)
@@ -438,11 +451,11 @@ def tile_mlcablock_pb_kernel(
             second_residual(1)
             fc1_bank(2)
             fc1_bank(3)
+            fc1_bank(1)
             quantise_x2(0)
             start_turned(0, 2)
-            quantise_sctx_pair(2)
-            fc1_bank(1)
             pair_is_quantised(0)
+            quantise_sctx_pair(2)
             quantise_sctx_pair(3)
             finish_on_vector(1)
             round_x2(1, nc.gpsimd)
@@ -467,11 +480,11 @@ def tile_mlcablock_pb_kernel(
             add_bias_in_psum(3)
             start_turned(1, 3)
             two_banks("scalar")
+            add_bias_to_two_banks()
             turn_x2(2)
             centre_and_gain(3, g_bc)
             second_residual(3)
             finish_turned(1, 3)
-            add_bias_to_two_banks()
             quantise_x2(2)
             pair_is_quantised(2)
             finish_two_banks("vector")
@@ -481,9 +494,10 @@ def tile_mlcablock_pb_kernel(
             two_banks("scalar")
             turn_x2(3)
             two_banks("scalar")
+            add_bias_to_two_banks()
             quantise_x2(3)
             pair_is_quantised(3)
-            two_banks("scalar")
+            finish_two_banks("vector")
             two_banks("scalar")
             two_banks("scalar")
             two_banks("scalar")

@@ -25,6 +25,7 @@ F_BANKS = F // BANK
 TURNED = {0: (2, 3), 1: (3,), 2: (), 3: ()}
 BANKS = 8
 ACC_BUFS = 3
+BANK_BUFS = 4
 AHEAD = ACC_BUFS
 H_BUFS = 10
 
@@ -101,7 +102,7 @@ def tile_mlcablock_pb_kernel(
 
         def turn_x2(j):
             x2_grouped = late.tile([P, 2 * P * 4], BF16, tag="x2_grouped", align_bytes=64)
-            turn_two_row_tiles(live["x2_bf", j], 0, x2_grouped)
+            turn_two_row_tiles(live["x2_bf", j], 0, x2_grouped, tag="gain", bufs=1)
             live["x2_grouped", j] = x2_grouped
 
         def turn_x2_direct(j):
@@ -110,7 +111,7 @@ def tile_mlcablock_pb_kernel(
             x2_grouped = late.tile([P, 2 * P * 4], BF16, tag="x2_grouped", align_bytes=64)
             for k in range(2):
                 columns = x2[:, k, :].rearrange("p (u c e) -> p u e c", u=2, e=2)
-                turned = psum.tile([P, 4, P], F32, tag="bank", bufs=BANKS - ACC_BUFS)
+                turned = psum.tile([P, 4, P], F32, tag="bank", bufs=BANK_BUFS)
                 for u in range(2):
                     for e in range(2):
                         nc.tensor.transpose(turned[:, 2 * u + e, :], columns[:, u, e, :], ident[:])
@@ -206,7 +207,7 @@ def tile_mlcablock_pb_kernel(
         def start_turned(j, c):
             h_turned = late.tile([P, F_BANKS, 2 * P], F32, tag="h_turned")
             for half in range(2):
-                acc = psum.tile([P, 2, 2 * P], F32, tag="bank", bufs=BANKS - ACC_BUFS)
+                acc = psum.tile([P, 2, 2 * P], F32, tag="bank", bufs=BANK_BUFS)
                 for e in range(2):
                     first = c * BANK + (2 * half + e) * P
                     nc.tensor.matmul_mx(
@@ -229,7 +230,7 @@ def tile_mlcablock_pb_kernel(
         def finish_turned(j, c):
             h_sb = hout.tile([P, 2, BANK], F32, tag="h_sb")
             for k in range(2):
-                back = psum.tile([P, F_BANKS, P], F32, tag="bank", bufs=BANKS - ACC_BUFS)
+                back = psum.tile([P, F_BANKS, P], F32, tag="bank", bufs=BANK_BUFS)
                 for r in range(F_BANKS):
                     nc.tensor.transpose(back[:, r, :], live["h_turned", j, c][:, r, k * P : (k + 1) * P], ident[:])
                 nc.scalar.copy(out=h_sb[:, k, :], in_=back[:].rearrange("p r c -> p (r c)"))
@@ -287,7 +288,7 @@ def tile_mlcablock_pb_kernel(
             fc1_grouped = prep.tile([P, F * 4], BF16, align_bytes=64)
 
             def turn_vectors():
-                turned = psum.tile([P, F_BANKS, P], BF16, tag="bank", bufs=BANKS - ACC_BUFS)
+                turned = psum.tile([P, F_BANKS, P], BF16, tag="bank", bufs=BANK_BUFS)
                 for r in range(F_BANKS):
                     nc.tensor.transpose(turned[:, r, :], ln_rows[:, r * P : (r + 1) * P], ident_bf[:])
                 nc.scalar.copy(out=vec_cols[:], in_=turned[:, :, 0:VECTORS])
@@ -300,8 +301,8 @@ def tile_mlcablock_pb_kernel(
                     )
                 return spread
 
-            def turn_two_row_tiles(rows_sb, r0, grouped, copy=nc.scalar.copy):
-                turned = psum.tile([P, 2, 2, P], F32, tag="bank", bufs=BANKS - ACC_BUFS)
+            def turn_two_row_tiles(rows_sb, r0, grouped, copy=nc.scalar.copy, tag="bank", bufs=BANK_BUFS):
+                turned = psum.tile([P, 2, 2, P], F32, tag=tag, bufs=bufs)
                 for r in range(2):
                     words = rows_sb[:, r0 + r, :].bitcast(F32)
                     for u in range(2):
@@ -333,7 +334,7 @@ def tile_mlcablock_pb_kernel(
                 i = 2 * j + k
                 engine.tensor_tensor(out=xb_out[:, i, :], in0=x_sb[:, i, :], in1=bias, op=ADD)
 
-            def add_bias_in_psum(j, tag="bank", bufs=BANKS - ACC_BUFS):
+            def add_bias_in_psum(j, tag="bank", bufs=BANK_BUFS):
                 for k in range(2):
                     xb = psum.tile([P, D], F32, tag=tag, bufs=bufs)
                     nc.tensor.matmul(out=xb[:], lhsT=ident_bf[:], rhs=x_sb[:, 2 * j + k, :], start=True, stop=False)
@@ -355,7 +356,7 @@ def tile_mlcablock_pb_kernel(
                     out=norm["rstd"][:], in_=norm["sum_sq"][:], func=ACT.Abs_reciprocal_sqrt, bias=eps[:], scale=1.0 / D**3
                 )
 
-            def project(j, tag="bank", bufs=BANKS - ACC_BUFS):
+            def project(j, tag="bank", bufs=BANK_BUFS):
                 for k in range(2):
                     i = 2 * j + k
                     a = psum.tile([P, D], F32, tag=tag, bufs=bufs)
@@ -402,17 +403,17 @@ def tile_mlcablock_pb_kernel(
             turn_sctx_pair(0)
             quantise(wo_grouped, wo_codes, wo_scales, 0, D)
             turn_vectors()
-            bo_psum = spread_row(B_OUT, "bank", BANKS - ACC_BUFS)
+            bo_psum = spread_row(B_OUT, "bank", BANK_BUFS)
             quantise_sctx_pair(0)
-            nc.scalar.copy(out=bo_bc[:], in_=bo_psum[:])
-            turn_sctx_pair(1)
-            project(0, "acc", ACC_BUFS)
-            g_psum = spread_row(G_SP, "acc", ACC_BUFS)
             for k in range(2):
                 add_out_bias(nc.vector, 0, k, bo_psum[:])
-            for k in range(2):
-                add_out_bias(nc.vector, 1, k, bo_bc[:])
-            for j in range(2, PAIRS):
+            turn_sctx_pair(1)
+            nc.scalar.copy(out=bo_bc[:], in_=bo_psum[:])
+            g_psum = spread_row(G_SP, "gain", 1)
+            nc.scalar.copy(out=g_bc[:], in_=g_psum[:])
+            nc.scalar.copy(out=fc1b_col[:], in_=vec_cols[:, :, B_FC1 : B_FC1 + 2])
+            project(0, "acc", ACC_BUFS)
+            for j in range(1, PAIRS):
                 for k in range(2):
                     add_out_bias(nc.gpsimd, j, k, bo_bc[:])
             quantise_sctx_pair(1)
@@ -424,13 +425,9 @@ def tile_mlcablock_pb_kernel(
                 progress["allowed"] = banks_up_to[j]
                 start_banks(progress["finished"] + AHEAD)
 
-            turn_fc1_half_bank(0)
-            turn_fc1_half_bank(1)
             first_residual(0)
             project(1)
             turn_fc1_half_bank(0)
-            nc.scalar.copy(out=g_bc[:], in_=g_psum[:])
-            nc.scalar.copy(out=fc1b_col[:], in_=vec_cols[:, :, B_FC1 : B_FC1 + 2])
             centre_and_gain(0, g_psum)
             turn_fc1_half_bank(1)
             add_bias_in_psum(0, "acc", ACC_BUFS)
@@ -444,10 +441,9 @@ def tile_mlcablock_pb_kernel(
                 turn_fc1_half_bank(b)
             fc1_bank(0)
             finish_on_vector(0)
-            round_x2(0, nc.gpsimd)
+            turn_x2_direct(0)
             turn_sctx_pair(2)
             turn_sctx_pair(3)
-            turn_x2(0)
             second_residual(1)
             fc1_bank(2)
             fc1_bank(3)

@@ -31,8 +31,8 @@ H_BUFS = 10
 
 FLOPS = 2 * TOKENS * D * (D + F)
 
-B_OUT, G_SP, B_SP, B_FC1 = 0, 1, 2, 3
-VECTORS = 5
+B_OUT, G_SP, B_SP, G_2, B_2, B_FC1 = 0, 1, 2, 3, 4, 5
+VECTORS = 7
 
 
 def tile_mlcablock_pb_kernel(
@@ -157,29 +157,27 @@ def tile_mlcablock_pb_kernel(
                 live["acc", n] = acc
                 progress["started"] = n + 1
 
-        def two_banks(relu_engine):
-            add_bias_to_two_banks()
-            finish_two_banks(relu_engine)
+        def two_banks():
+            add_bias_to_bank()
+            add_bias_to_bank()
+            finish_two_banks()
 
-        def add_bias_to_two_banks():
+        def add_bias_to_bank():
             n = progress["finished"]
-            h_sb = hout.tile([P, 2, BANK], F32, tag="h_sb")
-            for e in range(2):
-                c = banks[n + e][2]
-                nc.vector.tensor_tensor(
-                    out=h_sb[:, e, :], in0=live["acc", n + e][:], in1=fc1b_bc[:, c * BANK : (c + 1) * BANK], op=ADD
-                )
-                start_banks(n + e + 1 + AHEAD)
-            live["h_sb"] = h_sb
-            progress["finished"] = n + 2
+            if n % 2 == 0:
+                h_sb = hout.tile([P, 2, BANK], F32, tag="h_sb")
+                live["h_sb"] = h_sb
+            c = banks[n][2]
+            nc.vector.tensor_tensor(
+                out=live["h_sb"][:, n % 2, :], in0=live["acc", n][:], in1=fc1b_bc[:, c * BANK : (c + 1) * BANK], op=ADD
+            )
+            progress["finished"] = n + 1
+            start_banks(n + 1 + AHEAD)
 
-        def finish_two_banks(relu_engine):
+        def finish_two_banks():
             n = progress["finished"] - 2
             h_sb = live["h_sb"]
-            if relu_engine == "scalar":
-                nc.scalar.activation(out=h_sb[:], in_=h_sb[:], func=ACT.Relu)
-            else:
-                nc.vector.tensor_scalar(out=h_sb[:], in0=h_sb[:], scalar1=0.0, scalar2=None, op0=MAX)
+            nc.scalar.activation(out=h_sb[:], in_=h_sb[:], func=ACT.Relu)
             j, k, c = banks[n]
             if banks[n + 1][1] != k:
                 nc.sync.dma_start(out=h_v[:, 2 * j : 2 * j + 2, c * BANK : (c + 1) * BANK], in_=h_sb[:])
@@ -261,7 +259,7 @@ def tile_mlcablock_pb_kernel(
             nc.sync.dma_start(out=wo_sb[:, 0:2, :], in_=wo_v[:, 0:2, :])
             nc.sync.dma_start(out=wo_sb[:, 2:4, :], in_=wo_v[:, 2:4, :])
             nc.sync.dma_start(out=sctx_sb[:, 0:2, :], in_=sctx_v[:, 0:2, :])
-            for n, vec in enumerate((out_proj_b, lnsp_g, lnsp_b)):
+            for n, vec in enumerate((out_proj_b, lnsp_g, lnsp_b, ln2_g, ln2_b)):
                 nc.sync.dma_start(out=ln_rows[n : n + 1, :], in_=vec.rearrange("(o d) -> o d", o=1))
             nc.sync.dma_start(out=ln_rows[B_FC1 : B_FC1 + 2, :], in_=fc1_b[2 * BANK : F].rearrange("(o d) -> o d", o=2))
             nc.sync.dma_start(out=x_sb[:, 0:2, :], in_=x_v[:, 0:2, :])
@@ -273,8 +271,6 @@ def tile_mlcablock_pb_kernel(
             load_fc1(2)
             load_fc1(3)
             nc.sync.dma_start(out=sctx_sb[:, 4:TILES, :], in_=sctx_v[:, 4:TILES, :])
-            nc.sync.dma_start(out=g2_bc[:], in_=ln2_g.partition_broadcast(P))
-            nc.sync.dma_start(out=b2_bc[:], in_=ln2_b.partition_broadcast(P))
             nc.sync.dma_start(out=fc1b_bc[:], in_=fc1_b.partition_broadcast(P))
 
             xb_out = prep.tile([P, TILES, D], F32)
@@ -413,6 +409,9 @@ def tile_mlcablock_pb_kernel(
             nc.scalar.copy(out=g_bc[:], in_=g_psum[:])
             nc.scalar.copy(out=fc1b_col[:], in_=vec_cols[:, :, B_FC1 : B_FC1 + 2])
             project(0, "acc", ACC_BUFS)
+            for n, spread_bc in ((G_2, g2_bc), (B_2, b2_bc)):
+                spread = spread_row(n, "bank", BANK_BUFS)
+                nc.scalar.copy(out=spread_bc[:], in_=spread[:])
             for j in range(1, PAIRS):
                 for k in range(2):
                     add_out_bias(nc.gpsimd, j, k, bo_bc[:])
@@ -457,11 +456,11 @@ def tile_mlcablock_pb_kernel(
             round_x2(1, nc.gpsimd)
             finish_turned(0, 2)
             project(2)
-            two_banks("scalar")
+            two_banks()
             first_residual(2)
             turn_x2(1)
             add_bias_in_psum(2)
-            two_banks("scalar")
+            two_banks()
             start_turned(0, 3)
             centre_and_gain(2, g_bc)
             quantise_x2(1)
@@ -470,31 +469,33 @@ def tile_mlcablock_pb_kernel(
             project(3)
             first_residual(3)
             finish_turned(0, 3)
-            two_banks("scalar")
+            two_banks()
             finish_on_vector(2)
             round_x2(2, nc.gpsimd)
             add_bias_in_psum(3)
             start_turned(1, 3)
-            two_banks("scalar")
-            add_bias_to_two_banks()
+            two_banks()
             turn_x2(2)
+            add_bias_to_bank()
             centre_and_gain(3, g_bc)
             second_residual(3)
             finish_turned(1, 3)
             quantise_x2(2)
             pair_is_quantised(2)
-            finish_two_banks("vector")
+            add_bias_to_bank()
+            finish_two_banks()
             finish_on_vector(3)
             round_x2(3, nc.gpsimd)
-            two_banks("scalar")
-            two_banks("scalar")
+            two_banks()
+            two_banks()
             turn_x2(3)
-            two_banks("scalar")
-            add_bias_to_two_banks()
+            two_banks()
+            add_bias_to_bank()
             quantise_x2(3)
             pair_is_quantised(3)
-            finish_two_banks("vector")
-            two_banks("scalar")
-            two_banks("scalar")
-            two_banks("scalar")
+            add_bias_to_bank()
+            finish_two_banks()
+            two_banks()
+            two_banks()
+            two_banks()
             last_two_banks()

@@ -31,8 +31,8 @@ H_BUFS = 10
 
 FLOPS = 2 * TOKENS * D * (D + F)
 
-B_OUT, G_SP, B_SP, G_2, B_2, B_FC1 = 0, 1, 2, 3, 4, 5
-VECTORS = 7
+B_OUT, G_SP, B_SP, B_FC1 = 0, 1, 2, 3
+VECTORS = 5
 
 
 def tile_mlcablock_pb_kernel(
@@ -82,17 +82,34 @@ def tile_mlcablock_pb_kernel(
 
         def finish_on_vector(j):
             centred = late.tile([P, 2, D], F32, tag="centred", bufs=1)
-            x2 = x2_of[j]
             for k in range(2):
-                nc.vector.scalar_tensor_tensor(
-                    out=centred[:, k, :], in0=v2_of[j][:, k, :], scalar=norm2[j]["neg_mean"][:, k : k + 1],
-                    in1=g2_bc[:], op0=ADD, op1=MULT,
-                )
+                centre_x2(j, k, centred)
             for k in range(2):
-                nc.vector.scalar_tensor_tensor(
-                    out=x2[:, k, :], in0=centred[:, k, :], scalar=norm2[j]["rstd"][:, k : k + 1],
-                    in1=b2_bc[:], op0=MULT, op1=ADD,
-                )
+                scale_x2(j, k, centred)
+
+        def finish_between_banks(j):
+            centred = late.tile([P, 2, D], F32, tag="centred", bufs=1)
+            live["x2_grouped", j] = late.tile([P, 2 * P * 4], BF16, tag="x2_grouped", align_bytes=64, name="x2_grouped")
+            for k in range(2):
+                centre_x2(j, k, centred)
+                add_bias_to_bank()
+                if k == 1:
+                    finish_two_banks()
+                scale_x2(j, k, centred)
+                turn_x2_tile(j, k)
+            store_x2(j)
+
+        def centre_x2(j, k, centred):
+            nc.vector.scalar_tensor_tensor(
+                out=centred[:, k, :], in0=v2_of[j][:, k, :], scalar=norm2[j]["neg_mean"][:, k : k + 1],
+                in1=g2_bc[:], op0=ADD, op1=MULT,
+            )
+
+        def scale_x2(j, k, centred):
+            nc.vector.scalar_tensor_tensor(
+                out=x2_of[j][:, k, :], in0=centred[:, k, :], scalar=norm2[j]["rstd"][:, k : k + 1],
+                in1=b2_bc[:], op0=MULT, op1=ADD,
+            )
 
         def round_x2(j, engine):
             nc.sync.dma_start(out=x2_v[:, 2 * j : 2 * j + 2, :], in_=x2_of[j][:])
@@ -105,21 +122,25 @@ def tile_mlcablock_pb_kernel(
             turn_two_row_tiles(live["x2_bf", j], 0, x2_grouped, tag="gain", bufs=1)
             live["x2_grouped", j] = x2_grouped
 
+        def store_x2(j):
+            nc.sync.dma_start(out=x2_v[:, 2 * j : 2 * j + 2, :], in_=x2_of[j][:])
+
         def turn_x2_direct(j):
-            x2 = x2_of[j]
-            nc.sync.dma_start(out=x2_v[:, 2 * j : 2 * j + 2, :], in_=x2[:])
-            x2_grouped = late.tile([P, 2 * P * 4], BF16, tag="x2_grouped", align_bytes=64)
+            store_x2(j)
+            live["x2_grouped", j] = late.tile([P, 2 * P * 4], BF16, tag="x2_grouped", align_bytes=64, name="x2_grouped")
             for k in range(2):
-                columns = x2[:, k, :].rearrange("p (u c e) -> p u e c", u=2, e=2)
-                turned = psum.tile([P, 4, P], F32, tag="bank", bufs=BANK_BUFS)
-                for u in range(2):
-                    for e in range(2):
-                        nc.tensor.transpose(turned[:, 2 * u + e, :], columns[:, u, e, :], ident[:])
-                nc.scalar.copy(
-                    out=x2_grouped[:, k * P * 4 : (k + 1) * P * 4].rearrange("p (c t) -> p c t", t=4),
-                    in_=turned[:].rearrange("p t c -> p c t"),
-                )
-            live["x2_grouped", j] = x2_grouped
+                turn_x2_tile(j, k)
+
+        def turn_x2_tile(j, k):
+            columns = x2_of[j][:, k, :].rearrange("p (u c e) -> p u e c", u=2, e=2)
+            turned = psum.tile([P, 4, P], F32, tag="bank", bufs=BANK_BUFS)
+            for u in range(2):
+                for e in range(2):
+                    nc.tensor.transpose(turned[:, 2 * u + e, :], columns[:, u, e, :], ident[:])
+            nc.scalar.copy(
+                out=live["x2_grouped", j][:, k * P * 4 : (k + 1) * P * 4].rearrange("p (c t) -> p c t", t=4),
+                in_=turned[:].rearrange("p t c -> p c t"),
+            )
 
         def quantise_x2(j):
             nc.vector.quantize_mx(
@@ -127,6 +148,15 @@ def tile_mlcablock_pb_kernel(
                 scales=x2_scales[j][:],
                 in_=live["x2_grouped", j][:],
             )
+
+        def quantise_x2_tile(j, k):
+            nc.vector.quantize_mx(
+                out=x2_codes[j][:, k * P : (k + 1) * P].bitcast(FP8X4),
+                scales=x2_scales[j][:, k * P : (k + 1) * P],
+                in_=live["x2_grouped", j][:, k * P * 4 : (k + 1) * P * 4],
+            )
+            progress["allowed"] = banks_up_to[j, k]
+            start_banks(progress["finished"] + AHEAD)
 
         banks = []
         banks_up_to = {}
@@ -138,6 +168,10 @@ def tile_mlcablock_pb_kernel(
             elif len(straight) == 4:
                 banks += [(j, k, c) for k in range(2) for c in straight[2:4]]
             banks_up_to[j] = len(banks)
+            if len(straight) == 4:
+                banks[-8:] = [(j, k, c) for k in range(2) for c in straight]
+                banks_up_to[j, 0] = len(banks) - 4
+            banks_up_to[j, 1] = len(banks)
         progress = {"started": 0, "finished": 0, "allowed": 0}
 
         def start_banks(upto):
@@ -259,7 +293,7 @@ def tile_mlcablock_pb_kernel(
             nc.sync.dma_start(out=wo_sb[:, 0:2, :], in_=wo_v[:, 0:2, :])
             nc.sync.dma_start(out=wo_sb[:, 2:4, :], in_=wo_v[:, 2:4, :])
             nc.sync.dma_start(out=sctx_sb[:, 0:2, :], in_=sctx_v[:, 0:2, :])
-            for n, vec in enumerate((out_proj_b, lnsp_g, lnsp_b, ln2_g, ln2_b)):
+            for n, vec in enumerate((out_proj_b, lnsp_g, lnsp_b)):
                 nc.sync.dma_start(out=ln_rows[n : n + 1, :], in_=vec.rearrange("(o d) -> o d", o=1))
             nc.sync.dma_start(out=ln_rows[B_FC1 : B_FC1 + 2, :], in_=fc1_b[2 * BANK : F].rearrange("(o d) -> o d", o=2))
             nc.sync.dma_start(out=x_sb[:, 0:2, :], in_=x_v[:, 0:2, :])
@@ -271,6 +305,8 @@ def tile_mlcablock_pb_kernel(
             load_fc1(2)
             load_fc1(3)
             nc.sync.dma_start(out=sctx_sb[:, 4:TILES, :], in_=sctx_v[:, 4:TILES, :])
+            nc.sync.dma_start(out=g2_bc[:], in_=ln2_g.partition_broadcast(P))
+            nc.sync.dma_start(out=b2_bc[:], in_=ln2_b.partition_broadcast(P))
             nc.sync.dma_start(out=fc1b_bc[:], in_=fc1_b.partition_broadcast(P))
 
             xb_out = prep.tile([P, TILES, D], F32)
@@ -409,13 +445,9 @@ def tile_mlcablock_pb_kernel(
             nc.scalar.copy(out=g_bc[:], in_=g_psum[:])
             nc.scalar.copy(out=fc1b_col[:], in_=vec_cols[:, :, B_FC1 : B_FC1 + 2])
             project(0, "acc", ACC_BUFS)
-            for n, spread_bc in ((G_2, g2_bc), (B_2, b2_bc)):
-                spread = spread_row(n, "bank", BANK_BUFS)
-                nc.scalar.copy(out=spread_bc[:], in_=spread[:])
-            for j in range(1, PAIRS):
+            for j in range(2, PAIRS):
                 for k in range(2):
                     add_out_bias(nc.gpsimd, j, k, bo_bc[:])
-            quantise_sctx_pair(1)
 
             def fc1_bank(c):
                 quantise(fc1_grouped, fc1_codes, fc1_scales, c * BANK, BANK)
@@ -424,8 +456,11 @@ def tile_mlcablock_pb_kernel(
                 progress["allowed"] = banks_up_to[j]
                 start_banks(progress["finished"] + AHEAD)
 
+            quantise_sctx_pair(1)
             first_residual(0)
             project(1)
+            for k in range(2):
+                add_out_bias(nc.vector, 1, k, bo_psum[:])
             turn_fc1_half_bank(0)
             centre_and_gain(0, g_psum)
             turn_fc1_half_bank(1)
@@ -441,24 +476,24 @@ def tile_mlcablock_pb_kernel(
             fc1_bank(0)
             finish_on_vector(0)
             turn_x2_direct(0)
+            second_residual(1)
             turn_sctx_pair(2)
             turn_sctx_pair(3)
-            second_residual(1)
             fc1_bank(2)
             fc1_bank(3)
             fc1_bank(1)
             quantise_x2(0)
             start_turned(0, 2)
             pair_is_quantised(0)
-            quantise_sctx_pair(2)
-            quantise_sctx_pair(3)
             finish_on_vector(1)
             round_x2(1, nc.gpsimd)
+            quantise_sctx_pair(2)
+            quantise_sctx_pair(3)
             finish_turned(0, 2)
             project(2)
             two_banks()
-            first_residual(2)
             turn_x2(1)
+            first_residual(2)
             add_bias_in_psum(2)
             two_banks()
             start_turned(0, 3)
@@ -467,9 +502,9 @@ def tile_mlcablock_pb_kernel(
             pair_is_quantised(1)
             second_residual(2)
             project(3)
-            first_residual(3)
             finish_turned(0, 3)
             two_banks()
+            first_residual(3)
             finish_on_vector(2)
             round_x2(2, nc.gpsimd)
             add_bias_in_psum(3)

from contextlib import ExitStack

import concourse.mybir as mybir
from concourse.masks import make_identity

F32 = mybir.dt.float32
BF16 = mybir.dt.bfloat16
U32 = mybir.dt.uint32
U8 = mybir.dt.uint8
FP8X4 = mybir.dt.float8_e4m3fn_x4
ADD = mybir.AluOpType.add
MULT = mybir.AluOpType.mult
MAX = mybir.AluOpType.max
ACT = mybir.ActivationFunctionType

P = 128
D = 512
F = 2048
TOKENS = 1024
EPS = 1e-5
TILES = TOKENS // P
PAIRS = TILES // 2
BANK = 512
F_BANKS = F // BANK
TURNED = {0: (2, 3), 1: (3,), 2: (), 3: ()}
BANKS = 8
ACC_BUFS = 3
BANK_BUFS = 4
AHEAD = ACC_BUFS
H_BUFS = 10

FLOPS = 2 * TOKENS * D * (D + F)

B_OUT, G_SP, B_SP, B_FC1 = 0, 1, 2, 3
VECTORS = 5


def tile_mlcablock_pb_kernel(
    tc, sctx, x_ln1, out_proj_w, out_proj_b, lnsp_g, lnsp_b, ln2_g, ln2_b, fc1_w, fc1_b, out_0, out_1
):
    nc = tc.nc

    sctx_v = sctx.flatten_outer_dims().rearrange("(p t) d -> p t d", t=TILES)
    x_v = x_ln1.flatten_outer_dims().rearrange("(p t) d -> p t d", t=TILES)
    x2_v = out_0.flatten_outer_dims().rearrange("(p t) d -> p t d", t=TILES)
    h_v = out_1.flatten_outer_dims().rearrange("(p t) f -> p t f", t=TILES)
    wo_v = out_proj_w.rearrange("(r p) k -> p r k", p=P)
    fc1_v = fc1_w.rearrange("(r p) k -> p r k", p=P)

    with ExitStack() as ctx:
        ctx.enter_context(tc.manual_schedule())
        psum = ctx.enter_context(tc.psum_pool(name="psum", bufs=8))
        keep = ctx.enter_context(tc.tile_pool(name="keep", bufs=1))
        late = ctx.enter_context(tc.tile_pool(name="late", bufs=2))

        fc1_codes = keep.tile([P, F], U32, align_bytes=64)
        fc1_scales = keep.tile([P, F], U8, align_bytes=64)
        fc1b_bc = keep.tile([P, F], BF16)
        fc1b_col = keep.tile([P, F_BANKS, 2], F32)
        bo_bc = keep.tile([P, D], BF16)
        g_bc = keep.tile([P, D], BF16)
        g2_bc = keep.tile([P, D], BF16)
        b2_bc = keep.tile([P, D], BF16)
        ident = keep.tile([P, P], F32)
        eps = keep.tile([P, 1], F32)
        x2_codes = {}
        x2_scales = {}
        v2_of = {}
        x2_of = {}
        norm1 = {}
        norm2 = {}
        for j in range(PAIRS):
            x2_codes[j] = keep.tile([P, 2 * P], U32, name="x2_codes_%d" % j, align_bytes=64)
            x2_scales[j] = keep.tile([P, 2 * P], U8, name="x2_scales_%d" % j, align_bytes=64)
            v2_of[j] = keep.tile([P, 2, D], F32, name="v2_%d" % j)
            x2_of[j] = keep.tile([P, 2, D], F32, name="x2_%d" % j)
            for norm, which in ((norm1, 1), (norm2, 2)):
                norm[j] = {}
                for what in ("total", "neg_mean", "sum_sq", "rstd"):
                    norm[j][what] = keep.tile([P, 2], F32, name="%s_%d_%d" % (what, which, j))
        live = {}

        def finish_on_vector(j):
            centred = late.tile([P, 2, D], F32, tag="centred", bufs=1)
            for k in range(2):
                centre_x2(j, k, centred)
            for k in range(2):
                scale_x2(j, k, centred)

        def finish_between_banks(j):
            centred = late.tile([P, 2, D], F32, tag="centred", bufs=1)
            live["x2_grouped", j] = late.tile([P, 2 * P * 4], BF16, tag="x2_grouped", align_bytes=64, name="x2_grouped")
            for k in range(2):
                centre_x2(j, k, centred)
                add_bias_to_bank()
                if k == 1:
                    finish_two_banks()
                scale_x2(j, k, centred)
                turn_x2_tile(j, k)
            store_x2(j)

        def centre_x2(j, k, centred):
            nc.vector.scalar_tensor_tensor(
                out=centred[:, k, :], in0=v2_of[j][:, k, :], scalar=norm2[j]["neg_mean"][:, k : k + 1],
                in1=g2_bc[:], op0=ADD, op1=MULT,
            )

        def scale_x2(j, k, centred):
            nc.vector.scalar_tensor_tensor(
                out=x2_of[j][:, k, :], in0=centred[:, k, :], scalar=norm2[j]["rstd"][:, k : k + 1],
                in1=b2_bc[:], op0=MULT, op1=ADD,
            )

        def round_x2(j, engine):
            nc.sync.dma_start(out=x2_v[:, 2 * j : 2 * j + 2, :], in_=x2_of[j][:])
            x2_bf = late.tile([P, 2, D], BF16, tag="x2_bf")
            engine.tensor_scalar(out=x2_bf[:], in0=x2_of[j][:], scalar1=1.0, scalar2=0.0, op0=MULT, op1=ADD)
            live["x2_bf", j] = x2_bf

        def turn_x2(j):
            x2_grouped = late.tile([P, 2 * P * 4], BF16, tag="x2_grouped", align_bytes=64)
            turn_two_row_tiles(live["x2_bf", j], 0, x2_grouped, tag="gain", bufs=1)
            live["x2_grouped", j] = x2_grouped

        def store_x2(j):
            nc.sync.dma_start(out=x2_v[:, 2 * j : 2 * j + 2, :], in_=x2_of[j][:])

        def turn_x2_direct(j):
            store_x2(j)
            live["x2_grouped", j] = late.tile([P, 2 * P * 4], BF16, tag="x2_grouped", align_bytes=64, name="x2_grouped")
            for k in range(2):
                turn_x2_tile(j, k)

        def turn_x2_tile(j, k):
            columns = x2_of[j][:, k, :].rearrange("p (u c e) -> p u e c", u=2, e=2)
            turned = psum.tile([P, 4, P], F32, tag="bank", bufs=BANK_BUFS)
            for u in range(2):
                for e in range(2):
                    nc.tensor.transpose(turned[:, 2 * u + e, :], columns[:, u, e, :], ident[:])
            nc.scalar.copy(
                out=live["x2_grouped", j][:, k * P * 4 : (k + 1) * P * 4].rearrange("p (c t) -> p c t", t=4),
                in_=turned[:].rearrange("p t c -> p c t"),
            )

        def quantise_x2(j):
            nc.vector.quantize_mx(
                out=x2_codes[j][:].bitcast(FP8X4),
                scales=x2_scales[j][:],
                in_=live["x2_grouped", j][:],
            )

        def quantise_x2_tile(j, k):
            nc.vector.quantize_mx(
                out=x2_codes[j][:, k * P : (k + 1) * P].bitcast(FP8X4),
                scales=x2_scales[j][:, k * P : (k + 1) * P],
                in_=live["x2_grouped", j][:, k * P * 4 : (k + 1) * P * 4],
            )
            progress["allowed"] = banks_up_to[j, k]
            start_banks(progress["finished"] + AHEAD)

        banks = []
        banks_up_to = {}
        for j in range(PAIRS):
            straight = [c for c in range(F_BANKS) if c not in TURNED[j]]
            banks += [(j, k, c) for k in range(2) for c in straight[0:2]]
            if len(straight) == 3:
                banks += [(j, k, straight[2]) for k in range(2)]
            elif len(straight) == 4:
                banks += [(j, k, c) for k in range(2) for c in straight[2:4]]
            banks_up_to[j] = len(banks)
            if len(straight) == 4:
                banks[-8:] = [(j, k, c) for k in range(2) for c in straight]
                banks_up_to[j, 0] = len(banks) - 4
            banks_up_to[j, 1] = len(banks)
        progress = {"started": 0, "finished": 0, "allowed": 0}

        def start_banks(upto):
            while progress["started"] < min(upto, progress["allowed"], len(banks)):
                n = progress["started"]
                j, k, c = banks[n]
                acc = psum.tile([P, BANK], F32, tag="acc", bufs=ACC_BUFS)
                nc.tensor.matmul_mx(
                    out=acc[:],
                    lhsT=x2_codes[j][:, k * P : (k + 1) * P].bitcast(FP8X4),
                    lhsT_scale=x2_scales[j][:, k * P : (k + 1) * P],
                    rhs=fc1_codes[:, c * BANK : (c + 1) * BANK].bitcast(FP8X4),
                    rhs_scale=fc1_scales[:, c * BANK : (c + 1) * BANK],
                    start=True,
                    stop=True,
                )
                live["acc", n] = acc
                progress["started"] = n + 1

        def two_banks():
            add_bias_to_bank()
            add_bias_to_bank()
            finish_two_banks()

        def add_bias_to_bank():
            n = progress["finished"]
            if n % 2 == 0:
                h_sb = hout.tile([P, 2, BANK], F32, tag="h_sb")
                live["h_sb"] = h_sb
            c = banks[n][2]
            nc.vector.tensor_tensor(
                out=live["h_sb"][:, n % 2, :], in0=live["acc", n][:], in1=fc1b_bc[:, c * BANK : (c + 1) * BANK], op=ADD
            )
            progress["finished"] = n + 1
            start_banks(n + 1 + AHEAD)

        def finish_two_banks():
            n = progress["finished"] - 2
            h_sb = live["h_sb"]
            nc.scalar.activation(out=h_sb[:], in_=h_sb[:], func=ACT.Relu)
            j, k, c = banks[n]
            if banks[n + 1][1] != k:
                nc.sync.dma_start(out=h_v[:, 2 * j : 2 * j + 2, c * BANK : (c + 1) * BANK], in_=h_sb[:])
            else:
                nc.sync.dma_start(
                    out=h_v[:, 2 * j + k, c * BANK : (c + 2) * BANK], in_=h_sb[:].rearrange("p b n -> p (b n)")
                )

        def last_two_banks():
            n = progress["finished"]
            h_sb = hout.tile([P, 2, BANK], F32, tag="h_sb")
            for e in range(2):
                j, k, c = banks[n + e]
                nc.vector.tensor_tensor(
                    out=h_sb[:, e, :], in0=live["acc", n + e][:], in1=fc1b_bc[:, c * BANK : (c + 1) * BANK], op=ADD
                )
                if e == 0:
                    nc.scalar.activation(out=h_sb[:, e, :], in_=h_sb[:, e, :], func=ACT.Relu)
                else:
                    nc.vector.tensor_scalar(
                        out=h_sb[:, e, :], in0=h_sb[:, e, :], scalar1=0.0, scalar2=None, op0=MAX
                    )
                nc.sync.dma_start(out=h_v[:, 2 * j + k, c * BANK : (c + 1) * BANK], in_=h_sb[:, e, :])

        def start_turned(j, c):
            h_turned = late.tile([P, F_BANKS, 2 * P], F32, tag="h_turned")
            for half in range(2):
                acc = psum.tile([P, 2, 2 * P], F32, tag="bank", bufs=BANK_BUFS)
                for e in range(2):
                    first = c * BANK + (2 * half + e) * P
                    nc.tensor.matmul_mx(
                        out=acc[:, e, :],
                        lhsT=fc1_codes[:, first : first + P].bitcast(FP8X4),
                        lhsT_scale=fc1_scales[:, first : first + P],
                        rhs=x2_codes[j][:].bitcast(FP8X4),
                        rhs_scale=x2_scales[j][:],
                        start=True,
                        stop=True,
                    )
                for e in range(2):
                    r = 2 * half + e
                    nc.scalar.activation(
                        out=h_turned[:, r, :], in_=acc[:, e, :], func=ACT.Relu, bias=fc1b_col[:, r, c - 2 : c - 1],
                        scale=1.0,
                    )
            live["h_turned", j, c] = h_turned

        def finish_turned(j, c):
            h_sb = hout.tile([P, 2, BANK], F32, tag="h_sb")
            for k in range(2):
                back = psum.tile([P, F_BANKS, P], F32, tag="bank", bufs=BANK_BUFS)
                for r in range(F_BANKS):
                    nc.tensor.transpose(back[:, r, :], live["h_turned", j, c][:, r, k * P : (k + 1) * P], ident[:])
                nc.scalar.copy(out=h_sb[:, k, :], in_=back[:].rearrange("p r c -> p (r c)"))
            nc.sync.dma_start(out=h_v[:, 2 * j : 2 * j + 2, c * BANK : (c + 1) * BANK], in_=h_sb[:])

        with ExitStack() as early:
            hout = early.enter_context(tc.tile_pool(name="hout", bufs=H_BUFS, reuse_waits="tile"))
            prep = early.enter_context(tc.tile_pool(name="prep", bufs=1))
            work = early.enter_context(tc.tile_pool(name="work", bufs=2))
            junk = early.enter_context(tc.tile_pool(name="junk", bufs=4))

            ln_rows = prep.tile([P, D], BF16)
            nc.vector.memset(ln_rows[:], 0.0)
            nc.vector.memset(eps[:], EPS)
            warm = prep.tile([P, 1], F32)
            nc.scalar.activation(out=warm[:], in_=eps[:], func=ACT.Abs_reciprocal_sqrt)
            make_identity(nc, ident[:])
            ident_bf = prep.tile([P, P], BF16)
            make_identity(nc, ident_bf[:])

            wo_sb = prep.tile([P, D // P, D], BF16)
            sctx_sb = prep.tile([P, TILES, D], BF16)
            x_sb = prep.tile([P, TILES, D], BF16)
            fc1_sb = prep.tile([P, F // P, D], BF16)
            def load_fc1(c):
                nc.sync.dma_start(out=fc1_sb[:, 4 * c : 4 * c + 4, :], in_=fc1_v[:, 4 * c : 4 * c + 4, :])

            nc.sync.dma_start(out=wo_sb[:, 0:2, :], in_=wo_v[:, 0:2, :])
            nc.sync.dma_start(out=wo_sb[:, 2:4, :], in_=wo_v[:, 2:4, :])
            nc.sync.dma_start(out=sctx_sb[:, 0:2, :], in_=sctx_v[:, 0:2, :])
            for n, vec in enumerate((out_proj_b, lnsp_g, lnsp_b)):
                nc.sync.dma_start(out=ln_rows[n : n + 1, :], in_=vec.rearrange("(o d) -> o d", o=1))
            nc.sync.dma_start(out=ln_rows[B_FC1 : B_FC1 + 2, :], in_=fc1_b[2 * BANK : F].rearrange("(o d) -> o d", o=2))
            nc.sync.dma_start(out=x_sb[:, 0:2, :], in_=x_v[:, 0:2, :])
            nc.sync.dma_start(out=sctx_sb[:, 2:4, :], in_=sctx_v[:, 2:4, :])
            nc.sync.dma_start(out=x_sb[:, 2:4, :], in_=x_v[:, 2:4, :])
            load_fc1(0)
            load_fc1(1)
            nc.sync.dma_start(out=x_sb[:, 4:TILES, :], in_=x_v[:, 4:TILES, :])
            load_fc1(2)
            load_fc1(3)
            nc.sync.dma_start(out=sctx_sb[:, 4:TILES, :], in_=sctx_v[:, 4:TILES, :])
            nc.sync.dma_start(out=g2_bc[:], in_=ln2_g.partition_broadcast(P))
            nc.sync.dma_start(out=b2_bc[:], in_=ln2_b.partition_broadcast(P))
            nc.sync.dma_start(out=fc1b_bc[:], in_=fc1_b.partition_broadcast(P))

            xb_out = prep.tile([P, TILES, D], F32)
            vec_cols = prep.tile([P, F_BANKS, VECTORS], BF16)
            wo_grouped = prep.tile([P, D * 4], BF16, align_bytes=64)
            wo_codes = prep.tile([P, D], U32, align_bytes=64)
            wo_scales = prep.tile([P, D], U8, align_bytes=64)
            sctx_grouped = prep.tile([P, TOKENS * 4], BF16, align_bytes=64)
            sctx_codes = prep.tile([P, TOKENS], U32, align_bytes=64)
            sctx_scales = prep.tile([P, TOKENS], U8, align_bytes=64)
            fc1_grouped = prep.tile([P, F * 4], BF16, align_bytes=64)

            def turn_vectors():
                turned = psum.tile([P, F_BANKS, P], BF16, tag="bank", bufs=BANK_BUFS)
                for r in range(F_BANKS):
                    nc.tensor.transpose(turned[:, r, :], ln_rows[:, r * P : (r + 1) * P], ident_bf[:])
                nc.scalar.copy(out=vec_cols[:], in_=turned[:, :, 0:VECTORS])

            def spread_row(n, tag, bufs):
                spread = psum.tile([P, D], BF16, tag=tag, bufs=bufs)
                for r in range(F_BANKS):
                    nc.tensor.transpose(
                        spread[:, r * P : (r + 1) * P], vec_cols[:, r, n : n + 1].to_broadcast([P, P]), ident_bf[:]
                    )
                return spread

            def turn_two_row_tiles(rows_sb, r0, grouped, copy=nc.scalar.copy, tag="bank", bufs=BANK_BUFS):
                turned = psum.tile([P, 2, 2, P], F32, tag=tag, bufs=bufs)
                for r in range(2):
                    words = rows_sb[:, r0 + r, :].bitcast(F32)
                    for u in range(2):
                        nc.tensor.transpose(turned[:, r, u, :], words[:, u * P : (u + 1) * P], ident[:])
                copy(
                    out=grouped[:, r0 * P * 4 : (r0 + 2) * P * 4]
                    .bitcast(F32)
                    .rearrange("p (r c u) -> p r c u", r=2, u=2),
                    in_=turned[:].rearrange("p r u c -> p r c u"),
                )

            def quantise(grouped, codes, scales, first, count):
                nc.vector.quantize_mx(
                    out=codes[:, first : first + count].bitcast(FP8X4),
                    scales=scales[:, first : first + count],
                    in_=grouped[:, 4 * first : 4 * (first + count)],
                )

            def turn_sctx_pair(j):
                turn_two_row_tiles(sctx_sb, 2 * j, sctx_grouped)

            def quantise_sctx_pair(j):
                quantise(sctx_grouped, sctx_codes, sctx_scales, 2 * j * P, 2 * P)

            def turn_fc1_half_bank(b):
                turn_two_row_tiles(fc1_sb, 2 * b, fc1_grouped)

            def add_out_bias(engine, j, k, bias):
                i = 2 * j + k
                engine.tensor_tensor(out=xb_out[:, i, :], in0=x_sb[:, i, :], in1=bias, op=ADD)

            def add_bias_in_psum(j, tag="bank", bufs=BANK_BUFS):
                for k in range(2):
                    xb = psum.tile([P, D], F32, tag=tag, bufs=bufs)
                    nc.tensor.matmul(out=xb[:], lhsT=ident_bf[:], rhs=x_sb[:, 2 * j + k, :], start=True, stop=False)
                    nc.tensor.matmul(
                        out=xb[:], lhsT=ident_bf[:, B_SP : B_SP + 1].to_broadcast([P, P]), rhs=ln_rows[:],
                        start=False, stop=True,
                    )
                    live["xb_sp", j, k] = xb[:]

            def statistics(norm, v):
                nc.scalar.mul(norm["neg_mean"][:], norm["total"][:], -1.0 / D)
                for k in range(2):
                    squares = junk.tile([P, D], BF16, tag="squares")
                    nc.scalar.activation(
                        out=squares[:], in_=v[:, k, :], func=ACT.Square, bias=norm["total"][:, k : k + 1],
                        scale=-1.0 * D, accum_out=norm["sum_sq"][:, k : k + 1],
                    )
                nc.scalar.activation(
                    out=norm["rstd"][:], in_=norm["sum_sq"][:], func=ACT.Abs_reciprocal_sqrt, bias=eps[:], scale=1.0 / D**3
                )

            def project(j, tag="bank", bufs=BANK_BUFS):
                for k in range(2):
                    i = 2 * j + k
                    a = psum.tile([P, D], F32, tag=tag, bufs=bufs)
                    nc.tensor.matmul_mx(
                        out=a[:],
                        lhsT=sctx_codes[:, i * P : (i + 1) * P].bitcast(FP8X4),
                        lhsT_scale=sctx_scales[:, i * P : (i + 1) * P],
                        rhs=wo_codes[:].bitcast(FP8X4),
                        rhs_scale=wo_scales[:],
                        start=True,
                        stop=True,
                    )
                    live["a", j, k] = a

            def first_residual(j):
                v1 = work.tile([P, 2, D], F32, tag="v1")
                for k in range(2):
                    nc.vector.scalar_tensor_tensor(
                        out=v1[:, k, :], in0=live["a", j, k][:], scalar=1.0, in1=xb_out[:, 2 * j + k, :], op0=MULT, op1=ADD,
                        accum_out=norm1[j]["total"][:, k : k + 1],
                    )
                statistics(norm1[j], v1)
                live["v1", j] = v1

            def centre_and_gain(j, gain):
                centred = work.tile([P, 2, D], F32, tag="centred")
                for k in range(2):
                    nc.vector.scalar_tensor_tensor(
                        out=centred[:, k, :], in0=live["v1", j][:, k, :], scalar=norm1[j]["neg_mean"][:, k : k + 1],
                        in1=gain[:], op0=ADD, op1=MULT,
                    )
                live["centred", j] = centred

            def second_residual(j):
                for k in range(2):
                    nc.vector.scalar_tensor_tensor(
                        out=v2_of[j][:, k, :], in0=live["centred", j][:, k, :], scalar=norm1[j]["rstd"][:, k : k + 1],
                        in1=live["xb_sp", j, k], op0=MULT, op1=ADD, accum_out=norm2[j]["total"][:, k : k + 1],
                    )
                statistics(norm2[j], v2_of[j])

            turn_two_row_tiles(wo_sb, 0, wo_grouped)
            turn_two_row_tiles(wo_sb, 2, wo_grouped, nc.vector.tensor_copy)
            turn_sctx_pair(0)
            quantise(wo_grouped, wo_codes, wo_scales, 0, D)
            turn_vectors()
            bo_psum = spread_row(B_OUT, "bank", BANK_BUFS)
            quantise_sctx_pair(0)
            for k in range(2):
                add_out_bias(nc.vector, 0, k, bo_psum[:])
            turn_sctx_pair(1)
            nc.scalar.copy(out=bo_bc[:], in_=bo_psum[:])
            g_psum = spread_row(G_SP, "gain", 1)
            nc.scalar.copy(out=g_bc[:], in_=g_psum[:])
            nc.scalar.copy(out=fc1b_col[:], in_=vec_cols[:, :, B_FC1 : B_FC1 + 2])
            project(0, "acc", ACC_BUFS)
            for j in range(2, PAIRS):
                for k in range(2):
                    add_out_bias(nc.gpsimd, j, k, bo_bc[:])

            def fc1_bank(c):
                quantise(fc1_grouped, fc1_codes, fc1_scales, c * BANK, BANK)

            def pair_is_quantised(j):
                progress["allowed"] = banks_up_to[j]
                start_banks(progress["finished"] + AHEAD)

            quantise_sctx_pair(1)
            first_residual(0)
            project(1)
            for k in range(2):
                add_out_bias(nc.vector, 1, k, bo_psum[:])
            turn_fc1_half_bank(0)
            centre_and_gain(0, g_psum)
            turn_fc1_half_bank(1)
            add_bias_in_psum(0, "acc", ACC_BUFS)
            first_residual(1)
            turn_fc1_half_bank(2)
            turn_fc1_half_bank(3)
            second_residual(0)
            centre_and_gain(1, g_psum)
            add_bias_in_psum(1, "acc", ACC_BUFS)
            for b in range(4, 8):
                turn_fc1_half_bank(b)
            fc1_bank(0)
            finish_on_vector(0)
            turn_x2_direct(0)
            second_residual(1)
            turn_sctx_pair(2)
            turn_sctx_pair(3)
            fc1_bank(2)
            fc1_bank(3)
            fc1_bank(1)
            quantise_x2(0)
            start_turned(0, 2)
            pair_is_quantised(0)
            finish_on_vector(1)
            round_x2(1, nc.gpsimd)
            quantise_sctx_pair(2)
            quantise_sctx_pair(3)
            finish_turned(0, 2)
            project(2)
            two_banks()
            turn_x2(1)
            first_residual(2)
            add_bias_in_psum(2)
            two_banks()
            start_turned(0, 3)
            centre_and_gain(2, g_bc)
            quantise_x2(1)
            pair_is_quantised(1)
            second_residual(2)
            project(3)
            finish_turned(0, 3)
            two_banks()
            first_residual(3)
            finish_on_vector(2)
            round_x2(2, nc.gpsimd)
            add_bias_in_psum(3)
            start_turned(1, 3)
            two_banks()
            turn_x2(2)
            add_bias_to_bank()
            centre_and_gain(3, g_bc)
            second_residual(3)
            finish_turned(1, 3)
            quantise_x2(2)
            pair_is_quantised(2)
            add_bias_to_bank()
            finish_two_banks()
            finish_on_vector(3)
            round_x2(3, nc.gpsimd)
            two_banks()
            two_banks()
            turn_x2(3)
            two_banks()
            add_bias_to_bank()
            quantise_x2(3)
            pair_is_quantised(3)
            add_bias_to_bank()
            finish_two_banks()
            two_banks()
            two_banks()
            two_banks()
            last_two_banks()
